import numpy as np
import ml_dtypes


def mxq(x, axis, fmt="e4m3"):
    dtype, down = {"e4m3": (ml_dtypes.float8_e4m3fn, 7), "e5m2": (ml_dtypes.float8_e5m2, 14)}[fmt]
    v = np.moveaxis(np.asarray(x, np.float32).astype(ml_dtypes.bfloat16).astype(np.float64), axis, -1)
    blocks = v.reshape(v.shape[:-1] + (-1, 32))
    amax = np.abs(blocks).max(-1, keepdims=True)
    byte = np.maximum(np.where(amax > 0, np.frexp(amax)[1] - 1 + 127, 0) - down, 1)
    scale = np.exp2(byte - 127.0)
    codes = (blocks / scale).astype(np.float32).astype(dtype).astype(np.float64)
    return np.moveaxis((codes * scale).reshape(v.shape), -1, axis)


WIDE = False


def mx_kscale(k):
    if not WIDE:
        return np.ones(k)
    levels = np.array([10, -10, 5, -5, 0])
    a = np.random.permutation(np.resize(levels, k // 512 * 4)).reshape(k // 512, 4)
    idx = np.arange(k)
    return np.exp2(a[idx // 512, idx % 128 // 32])


BF16 = ml_dtypes.bfloat16


def bf(x):
    return np.asarray(x, np.float32).astype(BF16)


def f64(x):
    return np.asarray(x).astype(np.float64)


E2M1 = np.array([0.0, 0.5, 1.0, 1.5, 2.0, 3.0, 4.0, 6.0, -0.0, -0.5, -1.0, -1.5, -2.0, -3.0, -4.0, -6.0])


def pack_weight(w, fmt):
    k, n = w.shape
    w = f64(bf(w)).reshape(k // 32, 32, n)
    amax = np.abs(w).max(1)
    if fmt == "e4m3":
        byte = np.frexp(amax)[1] - 1 + 127 - 7
    else:
        mant, ex = np.frexp(amax / 6.0)
        byte = np.where(mant > 0.5, ex, ex - 1) + 127
    byte = np.clip(np.where(amax > 0, byte, 1), 1, 254)
    scaled = (w * np.exp2(127.0 - byte)[:, None, :]).reshape(k, n).astype(np.float32)
    by_word = np.ascontiguousarray(scaled.reshape(k // 512, 128, 4, n).transpose(0, 1, 3, 2))
    if fmt == "e4m3":
        words = by_word.astype(ml_dtypes.float8_e4m3fn).view(np.uint8)
    else:
        c = by_word.astype(ml_dtypes.float4_e2m1fn).view(np.uint8) & 0xF
        words = c[..., 0::2] | (c[..., 1::2] << 4)
    return np.ascontiguousarray(words), np.ascontiguousarray(byte.astype(np.uint8).reshape(k // 512, 16, n))


def unpack_weight(words, scales, fmt):
    g, p, n, _ = words.shape
    if fmt == "e4m3":
        vals = np.ascontiguousarray(words).view(ml_dtypes.float8_e4m3fn).astype(np.float64)
    else:
        nib = np.empty((g, p, n, 4), np.uint8)
        nib[..., 0::2] = words & 0xF
        nib[..., 1::2] = words >> 4
        vals = E2M1[nib]
    vals = vals * np.repeat(np.exp2(scales.astype(np.float64) - 127.0), 8, axis=1)[..., None]
    return vals.transpose(0, 1, 3, 2).reshape(g * 512, n)


B, N, F, U, S = 2, 2048, 128, 128, 2
C = S * (F + U)
FMT = "e4m3"


def sigmoid(v):
    return 1.0 / (1.0 + np.exp(-v))


def random_walk():
    a = np.random.uniform(size=(N, N))
    return a / a.sum(axis=1, keepdims=True) * np.sqrt(N)


def setup_inputs():
    s = mx_kscale(N)
    r_prev = bf(sigmoid(np.random.standard_normal((B, U, N))) * np.random.standard_normal((B, U, N)) * s)
    h_diff = bf(np.random.standard_normal((B, N, S * F)))
    u = bf(sigmoid(np.random.standard_normal((B, N, U))))
    state = bf(np.random.standard_normal((B, U * N)))
    s0_words, s0_scales = pack_weight(np.ascontiguousarray((random_walk() / s[None, :]).T), FMT)
    s1_words, s1_scales = pack_weight(np.ascontiguousarray((random_walk() / s[None, :]).T), FMT)
    ck_words, ck_scales = pack_weight(np.random.standard_normal((C, U)) / np.sqrt(C), FMT)
    return {"r_prev": r_prev,
            "h_diff": h_diff,
            "u": u,
            "state": state,
            "support0_words": s0_words,
            "support0_scales": s0_scales,
            "support1_words": s1_words,
            "support1_scales": s1_scales,
            "c_kernel_words": ck_words,
            "c_kernel_scales": ck_scales}


def diffuse(xq, supq):
    return np.concatenate([(xq @ sq.T) for sq in supq], axis=1)


def reference(r_prev, h_diff, u, state, support0_words, support0_scales, support1_words, support1_scales, c_kernel_words, c_kernel_scales):
    supq = (unpack_weight(support0_words, support0_scales, FMT).T, unpack_weight(support1_words, support1_scales, FMT).T)
    c_state = diffuse(mxq(f64(r_prev), 2, "e4m3"), supq).transpose(0, 2, 1)
    hc = np.concatenate([f64(h_diff), c_state], axis=-1)
    c = np.tanh(mxq(hc, 2, "e4m3") @ unpack_weight(c_kernel_words, c_kernel_scales, FMT))
    prev_t = f64(state).reshape(B, U, N).transpose(0, 2, 1)
    ug = f64(u)
    z = ug * prev_t + (1.0 - ug) * c
    return z.reshape(B, U * N)

@@ -1,0 +1,258 @@
+from contextlib import ExitStack
+
+import concourse.mybir as mybir
+from concourse.masks import make_identity
+
+F32 = mybir.dt.float32
+BF16 = mybir.dt.bfloat16
+I32 = mybir.dt.int32
+U32 = mybir.dt.uint32
+U8 = mybir.dt.uint8
+FP8X4 = mybir.dt.float8_e4m3fn_x4
+
+P = 128
+PACK = 4
+K_PASS = P * PACK
+BATCH = 2
+NODES = 2048
+UNITS = 128
+SUPPORTS = 2
+FEATS = 256
+CHANNELS = FEATS + SUPPORTS * UNITS
+PASSES = NODES // K_PASS
+CHUNK = 512
+CHUNKS = NODES // CHUNK
+TILES = CHUNK // P
+GROUP = 2
+ROUNDS = TILES // GROUP
+PAIRS = GROUP // 2
+SPAN = 2 * P // GROUP
+HALF = TILES * BATCH // 2
+HALF_BATCHES = HALF // GROUP
+
+FLOPS = 2 * BATCH * UNITS * NODES * NODES * SUPPORTS + 2 * BATCH * NODES * CHANNELS * UNITS
+
+
+def tile_gcrnncell_pb_kernel(
+    tc,
+    r_prev,
+    h_diff,
+    u,
+    state,
+    support0_words,
+    support0_scales,
+    support1_words,
+    support1_scales,
+    c_kernel_words,
+    c_kernel_scales,
+    out,
+):
+    nc = tc.nc
+    support_words = (support0_words, support1_words)
+    support_scales = (support0_scales, support1_scales)
+    tanh = mybir.ActivationFunctionType.Tanh
+    alu = mybir.AluOpType
+
+    with ExitStack() as ctx:
+        ctx.enter_context(tc.manual_schedule())
+        keep = ctx.enter_context(tc.tile_pool(name="keep", bufs=1))
+        ring = ctx.enter_context(tc.tile_pool(name="ring", bufs=2))
+        psum = ctx.enter_context(tc.psum_pool(name="psum", bufs=1))
+
+        identity = keep.tile([P, P], F32)
+        make_identity(nc, identity[:])
+        w_plane = [
+            keep.tile([P, NODES], U8, name="w_plane%d" % i, align_bytes=64) for i in range(SUPPORTS)
+        ]
+        ck_plane = keep.tile([P, UNITS], U8, align_bytes=64)
+        for i in range(SUPPORTS):
+            nc.vector.memset(w_plane[i][:].bitcast(I32), 0)
+        nc.vector.memset(ck_plane[:].bitcast(I32), 0)
+
+        r_sb = keep.tile([P, BATCH, NODES], BF16)
+        for b in range(BATCH):
+            nc.sync.dma_start(out=r_sb[:, b, :], in_=r_prev[b])
+        for i in range(SUPPORTS):
+            for quad in range(4):
+                nc.sync.dma_start(
+                    out=w_plane[i][32 * quad : 32 * quad + 16, :].bitcast(I32),
+                    in_=support_scales[i][:, 4 * quad : 4 * quad + 4, :].bitcast(I32),
+                )
+        ck_words = keep.tile([P, UNITS], U32, align_bytes=64)
+        nc.sync.dma_start(
+            out=ck_words[:].bitcast(I32),
+            in_=c_kernel_words[0].rearrange("p n t -> p (n t)").bitcast(I32),
+        )
+        for quad in range(4):
+            nc.sync.dma_start(
+                out=ck_plane[32 * quad : 32 * quad + 4, :].bitcast(I32),
+                in_=c_kernel_scales[0, 4 * quad : 4 * quad + 4, :].bitcast(I32),
+            )
+        w_words = {}
+        hc = {}
+        state_sb = {}
+        u_sb = {}
+        for c in range(CHUNKS):
+            nodes = slice(c * CHUNK, (c + 1) * CHUNK)
+            for i in range(SUPPORTS):
+                w_words[i, c] = keep.tile(
+                    [P, PASSES, CHUNK], U32, name="w_words%d_%d" % (i, c), align_bytes=64
+                )
+                nc.sync.dma_start(
+                    out=w_words[i, c][:].bitcast(I32),
+                    in_=support_words[i].rearrange("g p n t -> p g (n t)").bitcast(I32)[:, :, nodes],
+                )
+            hc[c] = keep.tile([P, TILES, BATCH, CHANNELS], BF16, name="hc%d" % c)
+            for b in range(BATCH):
+                nc.sync.dma_start(
+                    out=hc[c][:, :, b, 0:FEATS],
+                    in_=h_diff[b, nodes, :].rearrange("(t x) f -> x t f", x=P),
+                )
+            state_sb[c] = keep.tile([P, BATCH, CHUNK], BF16, name="state%d" % c)
+            nc.sync.dma_start(
+                out=state_sb[c][:],
+                in_=state.rearrange("b (k n) -> k b n", n=NODES)[:, :, nodes],
+            )
+            u_sb[c] = keep.tile([P, ROUNDS, BATCH, GROUP * UNITS], BF16, name="u%d" % c)
+            for b in range(BATCH):
+                nc.sync.dma_start(
+                    out=u_sb[c][:, :, b, :],
+                    in_=u[b, nodes, :].rearrange("(r x j) k -> x r (j k)", x=P, j=GROUP),
+                )
+        out_view = out.rearrange("b (c r x f) -> c r x b f", c=CHUNKS, r=ROUNDS, x=P)
+
+        r_grouped = keep.tile([P, PASSES, BATCH * UNITS, PACK], BF16, align_bytes=64)
+        r_words = keep.tile([P, PASSES, BATCH * UNITS], U32, align_bytes=64)
+        r_plane = keep.tile([P, PASSES, BATCH * UNITS], U8, align_bytes=64)
+        for g in range(PASSES):
+            r_flipped = psum.tile([P, 2, BATCH, UNITS], F32, tag="diffused", bufs=TILES)
+            for b in range(BATCH):
+                for half in range(2):
+                    nc.tensor.transpose(
+                        r_flipped[:, half, b, :],
+                        r_sb[:, b, :].bitcast(F32)[:, 256 * g + half : 256 * (g + 1) : 2],
+                        identity[:],
+                    )
+            copy = nc.vector.tensor_copy if g % 2 == 0 else nc.scalar.copy
+            copy(
+                out=r_grouped[:, g].bitcast(F32),
+                in_=r_flipped[:].rearrange("p h b k -> p (b k) h"),
+            )
+        for g in range(PASSES):
+            nc.vector.quantize_mx(
+                out=r_words[:, g, :].bitcast(FP8X4),
+                scales=r_plane[:, g, :],
+                in_=r_grouped[:, g].rearrange("p c t -> p (c t)"),
+            )
+
+        for c in range(CHUNKS):
+            diffused = [
+                psum.tile(
+                    [P, SUPPORTS, BATCH * UNITS], F32, tag="diffused", bufs=TILES, name="diffused%d" % t
+                )
+                for t in range(TILES)
+            ]
+            for i in range(SUPPORTS):
+                for t in range(TILES):
+                    for g in range(PASSES):
+                        nc.tensor.matmul_mx(
+                            out=diffused[t][:, i, :],
+                            lhsT=w_words[i, c][:, g, t * P : (t + 1) * P].bitcast(FP8X4),
+                            lhsT_scale=w_plane[i][4 * g : P, c * CHUNK + t * P : c * CHUNK + (t + 1) * P],
+                            rhs=r_words[:, g, :].bitcast(FP8X4),
+                            rhs_scale=r_plane[:, g, :],
+                            start=(g == 0),
+                            stop=(g == PASSES - 1),
+                        )
+            for t in range(TILES):
+                nc.scalar.copy(
+                    out=hc[c][:, t, :, FEATS:CHANNELS].rearrange("p b (i k) -> p b i k", i=SUPPORTS),
+                    in_=diffused[t][:].rearrange("p i (b k) -> p b i k", b=BATCH),
+                )
+
+            grouped = ring.tile([P, ROUNDS, BATCH, GROUP, P, PACK], BF16, align_bytes=64)
+            hc_words = ring.tile([P, ROUNDS, BATCH, GROUP, P], U32, align_bytes=64)
+            hc_plane = ring.tile([P, ROUNDS, BATCH, GROUP, P], U8, align_bytes=64)
+            for r in range(ROUNDS):
+                for b in range(BATCH):
+                    for pair in range(PAIRS):
+                        flipped = psum.tile([P, 2, 2 * P], F32, tag="flipped", bufs=2)
+                        for t in range(2):
+                            for half in range(2):
+                                nc.tensor.transpose(
+                                    flipped[:, half, t * P : (t + 1) * P],
+                                    hc[c][:, GROUP * r + 2 * pair + t, b, :].bitcast(F32)[
+                                        :, half : CHANNELS // 2 : 2
+                                    ],
+                                    identity[:],
+                                )
+                        copy = nc.vector.tensor_copy if b == 0 else nc.scalar.copy
+                        copy(
+                            out=grouped[:, r, b, :, SPAN * pair : SPAN * (pair + 1), :].bitcast(F32),
+                            in_=flipped[:].rearrange("p h (x j) -> p j x h", j=GROUP),
+                        )
+                for b in range(BATCH):
+                    nc.vector.quantize_mx(
+                        out=hc_words[:, r, b].rearrange("p j x -> p (j x)").bitcast(FP8X4),
+                        scales=hc_plane[:, r, b].rearrange("p j x -> p (j x)"),
+                        in_=grouped[:, r, b].rearrange("p j x t -> p (j x t)"),
+                    )
+
+            prev = psum.tile([P, ROUNDS, BATCH, PAIRS, UNITS], F32, tag="prev", bufs=1)
+            for r in range(ROUNDS):
+                for b in range(BATCH):
+                    for s in range(PAIRS):
+                        nc.tensor.transpose(
+                            prev[:, r, b, s, :],
+                            state_sb[c][:, b, :].bitcast(F32)[
+                                :, P * PAIRS * r + s : P * PAIRS * (r + 1) : PAIRS
+                            ],
+                            identity[:],
+                        )
+            u_flat = u_sb[c][:].rearrange("p r b f -> p (r b f)")
+            kept = ring.tile([P, TILES * BATCH * UNITS], F32)
+            nc.vector.tensor_tensor(
+                out=kept[:].rearrange("p (n e k) -> p n e k", e=2, k=UNITS),
+                in0=prev[:]
+                .rearrange("p r b s k -> p (r b s k)")
+                .bitcast(BF16)
+                .rearrange("p (n k e) -> p n e k", e=2, k=UNITS),
+                in1=u_flat.rearrange("p (n e k) -> p n e k", e=2, k=UNITS),
+                op=alu.mult,
+            )
+
+            for half in range(2):
+                cols = slice(half * HALF * UNITS, (half + 1) * HALF * UNITS)
+                product = psum.tile([P, HALF, UNITS], F32, tag="product", bufs=1)
+                for n in range(HALF):
+                    slot = half * HALF + n
+                    nc.tensor.matmul_mx(
+                        out=product[:, n, :],
+                        lhsT=hc_words[:].rearrange("p r b j x -> p (r b j) x")[:, slot, :].bitcast(FP8X4),
+                        lhsT_scale=hc_plane[:].rearrange("p r b j x -> p (r b j) x")[:, slot, :],
+                        rhs=ck_words[:].bitcast(FP8X4),
+                        rhs_scale=ck_plane[:],
+                        start=True,
+                        stop=True,
+                    )
+                candidate = ring.tile([P, HALF * UNITS], F32)
+                nc.scalar.activation(
+                    out=candidate[:], in_=product[:].rearrange("p n k -> p (n k)"), func=tanh
+                )
+                lost = ring.tile([P, HALF * UNITS], F32)
+                nc.vector.scalar_tensor_tensor(
+                    out=lost[:],
+                    in0=u_flat[:, cols],
+                    scalar=1.0,
+                    in1=candidate[:],
+                    op0=alu.subtract,
+                    op1=alu.mult,
+                )
+                z = ring.tile([P, HALF * UNITS], F32, bufs=3)
+                nc.vector.tensor_sub(out=z[:], in0=kept[:, cols], in1=lost[:])
+                r = half * HALF_BATCHES // BATCH
+                b = half * HALF_BATCHES % BATCH
+                nc.sync.dma_start(
+                    out=out_view[c, r][:, b : b + HALF_BATCHES, :],
+                    in_=z[:].rearrange("p (b f) -> p b f", b=HALF_BATCHES),
+                )

@@ -22,13 +22,10 @@ CHANNELS = FEATS + SUPPORTS * UNITS
 PASSES = NODES // K_PASS
 CHUNK = 512
 CHUNKS = NODES // CHUNK
-TILES = CHUNK // P
-GROUP = 2
-ROUNDS = TILES // GROUP
-PAIRS = GROUP // 2
-SPAN = 2 * P // GROUP
-HALF = TILES * BATCH // 2
-HALF_BATCHES = HALF // GROUP
+PAIR = 2
+ROUND = PAIR * P
+ROUNDS = NODES // ROUND
+CHUNK_ROUNDS = CHUNK // ROUND
 
 FLOPS = 2 * BATCH * UNITS * NODES * NODES * SUPPORTS + 2 * BATCH * NODES * CHANNELS * UNITS
 
@@ -68,64 +65,87 @@ def tile_gcrnncell_pb_kernel(
         for i in range(SUPPORTS):
             nc.vector.memset(w_plane[i][:].bitcast(I32), 0)
         nc.vector.memset(ck_plane[:].bitcast(I32), 0)
+        warm = keep.tile([P, 1], F32)
+        nc.vector.memset(warm[:], 0.0)
+        nc.scalar.activation(out=warm[:], in_=warm[:], func=tanh)
+
+        w_words = {}
+        hc = {}
+        state_sb = {}
+        u_sb = {}
+
+        def load_supports(c, pieces):
+            for i in range(SUPPORTS):
+                w_words[i, c] = keep.tile(
+                    [P, PASSES, CHUNK], U32, name="w_words%d_%d" % (i, c), align_bytes=64
+                )
+            width = CHUNK // pieces
+            for piece in range(pieces):
+                for i in range(SUPPORTS):
+                    nc.sync.dma_start(
+                        out=w_words[i, c][:, :, piece * width : (piece + 1) * width].bitcast(I32),
+                        in_=support_words[i]
+                        .rearrange("g p n t -> p g (n t)")
+                        .bitcast(I32)[:, :, c * CHUNK + piece * width : c * CHUNK + (piece + 1) * width],
+                    )
+
+        def load_features(c):
+            hc[c] = keep.tile([P, CHUNK // P, BATCH, CHANNELS], BF16, name="hc%d" % c)
+            for b in range(BATCH):
+                nc.sync.dma_start(
+                    out=hc[c][:, :, b, 0:FEATS],
+                    in_=h_diff[b, c * CHUNK : (c + 1) * CHUNK, :].rearrange("(t x) f -> x t f", x=P),
+                )
+
+        def load_gate(c):
+            state_sb[c] = keep.tile([P, BATCH, CHUNK], BF16, name="state%d" % c)
+            nc.sync.dma_start(
+                out=state_sb[c][:],
+                in_=state.rearrange("b (k n) -> k b n", n=NODES)[:, :, c * CHUNK : (c + 1) * CHUNK],
+            )
+            u_sb[c] = keep.tile([P, CHUNK_ROUNDS, BATCH, PAIR * UNITS], BF16, name="u%d" % c)
+            for b in range(BATCH):
+                nc.sync.dma_start(
+                    out=u_sb[c][:, :, b, :],
+                    in_=u[b, c * CHUNK : (c + 1) * CHUNK, :].rearrange(
+                        "(r x j) k -> x r (j k)", x=P, j=PAIR
+                    ),
+                )
 
         r_sb = keep.tile([P, BATCH, NODES], BF16)
-        for b in range(BATCH):
-            nc.sync.dma_start(out=r_sb[:, b, :], in_=r_prev[b])
+        for part in range(2):
+            cols = slice(part * NODES // 2, (part + 1) * NODES // 2)
+            nc.sync.dma_start(out=r_sb[:, :, cols], in_=r_prev.rearrange("b k n -> k b n")[:, :, cols])
         for i in range(SUPPORTS):
             for quad in range(4):
                 nc.sync.dma_start(
                     out=w_plane[i][32 * quad : 32 * quad + 16, :].bitcast(I32),
                     in_=support_scales[i][:, 4 * quad : 4 * quad + 4, :].bitcast(I32),
                 )
+        load_supports(0, CHUNK_ROUNDS)
         ck_words = keep.tile([P, UNITS], U32, align_bytes=64)
-        nc.sync.dma_start(
-            out=ck_words[:].bitcast(I32),
-            in_=c_kernel_words[0].rearrange("p n t -> p (n t)").bitcast(I32),
-        )
-        for quad in range(4):
-            nc.sync.dma_start(
-                out=ck_plane[32 * quad : 32 * quad + 4, :].bitcast(I32),
-                in_=c_kernel_scales[0, 4 * quad : 4 * quad + 4, :].bitcast(I32),
-            )
-        w_words = {}
-        hc = {}
-        state_sb = {}
-        u_sb = {}
         for c in range(CHUNKS):
-            nodes = slice(c * CHUNK, (c + 1) * CHUNK)
-            for i in range(SUPPORTS):
-                w_words[i, c] = keep.tile(
-                    [P, PASSES, CHUNK], U32, name="w_words%d_%d" % (i, c), align_bytes=64
-                )
+            load_features(c)
+            if c == 0:
                 nc.sync.dma_start(
-                    out=w_words[i, c][:].bitcast(I32),
-                    in_=support_words[i].rearrange("g p n t -> p g (n t)").bitcast(I32)[:, :, nodes],
+                    out=ck_words[:].bitcast(I32),
+                    in_=c_kernel_words[0].rearrange("p n t -> p (n t)").bitcast(I32),
                 )
-            hc[c] = keep.tile([P, TILES, BATCH, CHANNELS], BF16, name="hc%d" % c)
-            for b in range(BATCH):
-                nc.sync.dma_start(
-                    out=hc[c][:, :, b, 0:FEATS],
-                    in_=h_diff[b, nodes, :].rearrange("(t x) f -> x t f", x=P),
-                )
-            state_sb[c] = keep.tile([P, BATCH, CHUNK], BF16, name="state%d" % c)
-            nc.sync.dma_start(
-                out=state_sb[c][:],
-                in_=state.rearrange("b (k n) -> k b n", n=NODES)[:, :, nodes],
-            )
-            u_sb[c] = keep.tile([P, ROUNDS, BATCH, GROUP * UNITS], BF16, name="u%d" % c)
-            for b in range(BATCH):
-                nc.sync.dma_start(
-                    out=u_sb[c][:, :, b, :],
-                    in_=u[b, nodes, :].rearrange("(r x j) k -> x r (j k)", x=P, j=GROUP),
-                )
-        out_view = out.rearrange("b (c r x f) -> c r x b f", c=CHUNKS, r=ROUNDS, x=P)
+                for quad in range(4):
+                    nc.sync.dma_start(
+                        out=ck_plane[32 * quad : 32 * quad + 4, :].bitcast(I32),
+                        in_=c_kernel_scales[0, 4 * quad : 4 * quad + 4, :].bitcast(I32),
+                    )
+            if c + 1 < CHUNKS:
+                load_supports(c + 1, 1)
+            load_gate(c)
+        out_view = out.rearrange("b (s x f) -> s x b f", s=ROUNDS, x=P)
 
         r_grouped = keep.tile([P, PASSES, BATCH * UNITS, PACK], BF16, align_bytes=64)
         r_words = keep.tile([P, PASSES, BATCH * UNITS], U32, align_bytes=64)
         r_plane = keep.tile([P, PASSES, BATCH * UNITS], U8, align_bytes=64)
         for g in range(PASSES):
-            r_flipped = psum.tile([P, 2, BATCH, UNITS], F32, tag="diffused", bufs=TILES)
+            r_flipped = psum.tile([P, 2, BATCH, UNITS], F32, tag="diffused", bufs=2 * PAIR)
             for b in range(BATCH):
                 for half in range(2):
                     nc.tensor.transpose(
@@ -145,114 +165,124 @@ def tile_gcrnncell_pb_kernel(
                 in_=r_grouped[:, g].rearrange("p c t -> p (c t)"),
             )
 
-        for c in range(CHUNKS):
+        hc_packed = {}
+        kept = {}
+
+        def diffuse(s):
+            c, r = divmod(s, CHUNK_ROUNDS)
             diffused = [
                 psum.tile(
-                    [P, SUPPORTS, BATCH * UNITS], F32, tag="diffused", bufs=TILES, name="diffused%d" % t
+                    [P, SUPPORTS, BATCH * UNITS], F32, tag="diffused", bufs=2 * PAIR, name="diffused"
                 )
-                for t in range(TILES)
+                for t in range(PAIR)
             ]
             for i in range(SUPPORTS):
-                for t in range(TILES):
+                for t in range(PAIR):
+                    first = (PAIR * r + t) * P
                     for g in range(PASSES):
                         nc.tensor.matmul_mx(
                             out=diffused[t][:, i, :],
-                            lhsT=w_words[i, c][:, g, t * P : (t + 1) * P].bitcast(FP8X4),
-                            lhsT_scale=w_plane[i][4 * g : P, c * CHUNK + t * P : c * CHUNK + (t + 1) * P],
+                            lhsT=w_words[i, c][:, g, first : first + P].bitcast(FP8X4),
+                            lhsT_scale=w_plane[i][4 * g : P, c * CHUNK + first : c * CHUNK + first + P],
                             rhs=r_words[:, g, :].bitcast(FP8X4),
                             rhs_scale=r_plane[:, g, :],
                             start=(g == 0),
                             stop=(g == PASSES - 1),
                         )
-            for t in range(TILES):
+            for t in range(PAIR):
                 nc.scalar.copy(
-                    out=hc[c][:, t, :, FEATS:CHANNELS].rearrange("p b (i k) -> p b i k", i=SUPPORTS),
+                    out=hc[c][:, PAIR * r + t, :, FEATS:CHANNELS].rearrange(
+                        "p b (i k) -> p b i k", i=SUPPORTS
+                    ),
                     in_=diffused[t][:].rearrange("p i (b k) -> p b i k", b=BATCH),
                 )
 
-            grouped = ring.tile([P, ROUNDS, BATCH, GROUP, P, PACK], BF16, align_bytes=64)
-            hc_words = ring.tile([P, ROUNDS, BATCH, GROUP, P], U32, align_bytes=64)
-            hc_plane = ring.tile([P, ROUNDS, BATCH, GROUP, P], U8, align_bytes=64)
-            for r in range(ROUNDS):
-                for b in range(BATCH):
-                    for pair in range(PAIRS):
-                        flipped = psum.tile([P, 2, 2 * P], F32, tag="flipped", bufs=2)
-                        for t in range(2):
-                            for half in range(2):
-                                nc.tensor.transpose(
-                                    flipped[:, half, t * P : (t + 1) * P],
-                                    hc[c][:, GROUP * r + 2 * pair + t, b, :].bitcast(F32)[
-                                        :, half : CHANNELS // 2 : 2
-                                    ],
-                                    identity[:],
-                                )
-                        copy = nc.vector.tensor_copy if b == 0 else nc.scalar.copy
-                        copy(
-                            out=grouped[:, r, b, :, SPAN * pair : SPAN * (pair + 1), :].bitcast(F32),
-                            in_=flipped[:].rearrange("p h (x j) -> p j x h", j=GROUP),
-                        )
-                for b in range(BATCH):
-                    nc.vector.quantize_mx(
-                        out=hc_words[:, r, b].rearrange("p j x -> p (j x)").bitcast(FP8X4),
-                        scales=hc_plane[:, r, b].rearrange("p j x -> p (j x)"),
-                        in_=grouped[:, r, b].rearrange("p j x t -> p (j x t)"),
-                    )
-
-            prev = psum.tile([P, ROUNDS, BATCH, PAIRS, UNITS], F32, tag="prev", bufs=1)
-            for r in range(ROUNDS):
-                for b in range(BATCH):
-                    for s in range(PAIRS):
+        def flip(s):
+            c, r = divmod(s, CHUNK_ROUNDS)
+            grouped = ring.tile([P, BATCH, PAIR, P, PACK], BF16, align_bytes=64)
+            hc_words = ring.tile([P, BATCH, PAIR, P], U32, align_bytes=64)
+            hc_plane = ring.tile([P, BATCH, PAIR, P], U8, align_bytes=64)
+            for b in range(BATCH):
+                flipped = psum.tile([P, 2, ROUND], F32, tag="flipped", bufs=2)
+                for t in range(PAIR):
+                    for half in range(2):
                         nc.tensor.transpose(
-                            prev[:, r, b, s, :],
-                            state_sb[c][:, b, :].bitcast(F32)[
-                                :, P * PAIRS * r + s : P * PAIRS * (r + 1) : PAIRS
-                            ],
+                            flipped[:, half, t * P : (t + 1) * P],
+                            hc[c][:, PAIR * r + t, b, :].bitcast(F32)[:, half : CHANNELS // 2 : 2],
                             identity[:],
                         )
-            u_flat = u_sb[c][:].rearrange("p r b f -> p (r b f)")
-            kept = ring.tile([P, TILES * BATCH * UNITS], F32)
+                copy = nc.vector.tensor_copy if b == 0 else nc.scalar.copy
+                copy(
+                    out=grouped[:, b].bitcast(F32),
+                    in_=flipped[:].rearrange("p h (x j) -> p j x h", j=PAIR),
+                )
+            for b in range(BATCH):
+                nc.vector.quantize_mx(
+                    out=hc_words[:, b].rearrange("p j x -> p (j x)").bitcast(FP8X4),
+                    scales=hc_plane[:, b].rearrange("p j x -> p (j x)"),
+                    in_=grouped[:, b].rearrange("p j x t -> p (j x t)"),
+                )
+            hc_packed[s] = (hc_words, hc_plane)
+
+        def recall(s):
+            c, r = divmod(s, CHUNK_ROUNDS)
+            prev = psum.tile([P, BATCH, UNITS], F32, tag="prev", bufs=1)
+            for b in range(BATCH):
+                nc.tensor.transpose(
+                    prev[:, b, :],
+                    state_sb[c][:, b, :].bitcast(F32)[:, r * P : (r + 1) * P],
+                    identity[:],
+                )
+            kept[s] = ring.tile([P, BATCH, PAIR, UNITS], F32, name="kept")
             nc.vector.tensor_tensor(
-                out=kept[:].rearrange("p (n e k) -> p n e k", e=2, k=UNITS),
+                out=kept[s][:],
                 in0=prev[:]
-                .rearrange("p r b s k -> p (r b s k)")
+                .rearrange("p b k -> p (b k)")
                 .bitcast(BF16)
-                .rearrange("p (n k e) -> p n e k", e=2, k=UNITS),
-                in1=u_flat.rearrange("p (n e k) -> p n e k", e=2, k=UNITS),
+                .rearrange("p (b k j) -> p b j k", b=BATCH, j=PAIR),
+                in1=u_sb[c][:, r].rearrange("p b (j k) -> p b j k", j=PAIR),
                 op=alu.mult,
             )
 
-            for half in range(2):
-                cols = slice(half * HALF * UNITS, (half + 1) * HALF * UNITS)
-                product = psum.tile([P, HALF, UNITS], F32, tag="product", bufs=1)
-                for n in range(HALF):
-                    slot = half * HALF + n
+        def candidate(s):
+            c, r = divmod(s, CHUNK_ROUNDS)
+            hc_words, hc_plane = hc_packed[s]
+            product = psum.tile([P, BATCH, PAIR, UNITS], F32, tag="product", bufs=1)
+            for b in range(BATCH):
+                for j in range(PAIR):
                     nc.tensor.matmul_mx(
-                        out=product[:, n, :],
-                        lhsT=hc_words[:].rearrange("p r b j x -> p (r b j) x")[:, slot, :].bitcast(FP8X4),
-                        lhsT_scale=hc_plane[:].rearrange("p r b j x -> p (r b j) x")[:, slot, :],
+                        out=product[:, b, j, :],
+                        lhsT=hc_words[:, b, j, :].bitcast(FP8X4),
+                        lhsT_scale=hc_plane[:, b, j, :],
                         rhs=ck_words[:].bitcast(FP8X4),
                         rhs_scale=ck_plane[:],
                         start=True,
                         stop=True,
                     )
-                candidate = ring.tile([P, HALF * UNITS], F32)
-                nc.scalar.activation(
-                    out=candidate[:], in_=product[:].rearrange("p n k -> p (n k)"), func=tanh
-                )
-                lost = ring.tile([P, HALF * UNITS], F32)
-                nc.vector.scalar_tensor_tensor(
-                    out=lost[:],
-                    in0=u_flat[:, cols],
-                    scalar=1.0,
-                    in1=candidate[:],
-                    op0=alu.subtract,
-                    op1=alu.mult,
-                )
-                z = ring.tile([P, HALF * UNITS], F32, bufs=3)
-                nc.vector.tensor_sub(out=z[:], in0=kept[:, cols], in1=lost[:])
-                r = half * HALF_BATCHES // BATCH
-                b = half * HALF_BATCHES % BATCH
-                nc.sync.dma_start(
-                    out=out_view[c, r][:, b : b + HALF_BATCHES, :],
-                    in_=z[:].rearrange("p (b f) -> p b f", b=HALF_BATCHES),
-                )
+            fresh = ring.tile([P, BATCH, PAIR * UNITS], F32)
+            nc.scalar.activation(
+                out=fresh[:], in_=product[:].rearrange("p b j k -> p b (j k)"), func=tanh
+            )
+            lost = ring.tile([P, BATCH, PAIR * UNITS], F32)
+            nc.vector.scalar_tensor_tensor(
+                out=lost[:],
+                in0=u_sb[c][:, r],
+                scalar=1.0,
+                in1=fresh[:],
+                op0=alu.subtract,
+                op1=alu.mult,
+            )
+            z = keep.tile([P, BATCH, PAIR * UNITS], F32, name="z%d" % s)
+            nc.vector.tensor_sub(
+                out=z[:], in0=kept[s][:].rearrange("p b j k -> p b (j k)"), in1=lost[:]
+            )
+            nc.sync.dma_start(out=out_view[s], in_=z[:])
+
+        for step in range(ROUNDS + 3):
+            if 0 <= step - 2 < ROUNDS:
+                flip(step - 2)
+            if 0 <= step - 3 < ROUNDS:
+                recall(step - 3)
+                candidate(step - 3)
+            if step < ROUNDS:
+                diffuse(step)

@@ -165,6 +165,7 @@ def tile_gcrnncell_pb_kernel(
                 in_=r_grouped[:, g].rearrange("p c t -> p (c t)"),
             )
 
+        hc_grouped = {}
         hc_packed = {}
         kept = {}
 
@@ -200,8 +201,6 @@ def tile_gcrnncell_pb_kernel(
         def flip(s):
             c, r = divmod(s, CHUNK_ROUNDS)
             grouped = ring.tile([P, BATCH, PAIR, P, PACK], BF16, align_bytes=64)
-            hc_words = ring.tile([P, BATCH, PAIR, P], U32, align_bytes=64)
-            hc_plane = ring.tile([P, BATCH, PAIR, P], U8, align_bytes=64)
             for b in range(BATCH):
                 flipped = psum.tile([P, 2, ROUND], F32, tag="flipped", bufs=2)
                 for t in range(PAIR):
@@ -216,6 +215,12 @@ def tile_gcrnncell_pb_kernel(
                     out=grouped[:, b].bitcast(F32),
                     in_=flipped[:].rearrange("p h (x j) -> p j x h", j=PAIR),
                 )
+            hc_grouped[s] = grouped
+
+        def pack(s):
+            grouped = hc_grouped[s]
+            hc_words = ring.tile([P, BATCH, PAIR, P], U32, align_bytes=64)
+            hc_plane = ring.tile([P, BATCH, PAIR, P], U8, align_bytes=64)
             for b in range(BATCH):
                 nc.vector.quantize_mx(
                     out=hc_words[:, b].rearrange("p j x -> p (j x)").bitcast(FP8X4),
@@ -273,8 +278,11 @@ def tile_gcrnncell_pb_kernel(
                 op1=alu.mult,
             )
             z = keep.tile([P, BATCH, PAIR * UNITS], F32, name="z%d" % s)
-            nc.vector.tensor_sub(
-                out=z[:], in0=kept[s][:].rearrange("p b j k -> p b (j k)"), in1=lost[:]
+            nc.gpsimd.tensor_tensor(
+                out=z[:],
+                in0=kept[s][:].rearrange("p b j k -> p b (j k)"),
+                in1=lost[:],
+                op=alu.subtract,
             )
             nc.sync.dma_start(out=out_view[s], in_=z[:])
 
@@ -283,6 +291,9 @@ def tile_gcrnncell_pb_kernel(
                 flip(step - 2)
             if 0 <= step - 3 < ROUNDS:
                 recall(step - 3)
+            if 0 <= step - 2 < ROUNDS:
+                pack(step - 2)
+            if 0 <= step - 3 < ROUNDS:
                 candidate(step - 3)
             if step < ROUNDS:
                 diffuse(step)

@@ -58,6 +58,11 @@ def tile_gcrnncell_pb_kernel(
 
         identity = keep.tile([P, P], F32)
         make_identity(nc, identity[:])
+        sorter = keep.tile([P, P], F32)
+        nc.vector.tensor_copy(
+            out=sorter[:].rearrange("p (u x e) -> p u x e", u=2, e=2),
+            in_=identity[:].rearrange("p (x u e) -> p u x e", u=2, e=2),
+        )
         w_plane = [
             keep.tile([P, NODES], U8, name="w_plane%d" % i, align_bytes=64) for i in range(SUPPORTS)
         ]
@@ -70,6 +75,7 @@ def tile_gcrnncell_pb_kernel(
         nc.scalar.activation(out=warm[:], in_=warm[:], func=tanh)
 
         w_words = {}
+        h_raw = {}
         hc = {}
         state_sb = {}
         u_sb = {}
@@ -90,10 +96,11 @@ def tile_gcrnncell_pb_kernel(
                     )
 
         def load_features(c):
-            hc[c] = keep.tile([P, CHUNK // P, BATCH, CHANNELS], BF16, name="hc%d" % c)
+            h_raw[c] = keep.tile([P, CHUNK // P, BATCH, FEATS], BF16, name="h_raw%d" % c)
+            hc[c] = keep.tile([P, CHUNK // P, BATCH, 2, CHANNELS // 2], BF16, name="hc%d" % c)
             for b in range(BATCH):
                 nc.sync.dma_start(
-                    out=hc[c][:, :, b, 0:FEATS],
+                    out=h_raw[c][:, :, b, :],
                     in_=h_diff[b, c * CHUNK : (c + 1) * CHUNK, :].rearrange("(t x) f -> x t f", x=P),
                 )
 
@@ -151,7 +158,7 @@ def tile_gcrnncell_pb_kernel(
                     nc.tensor.transpose(
                         r_flipped[:, half, b, :],
                         r_sb[:, b, :].bitcast(F32)[:, 256 * g + half : 256 * (g + 1) : 2],
-                        identity[:],
+                        sorter[:],
                     )
             copy = nc.vector.tensor_copy if g % 2 == 0 else nc.scalar.copy
             copy(
@@ -168,6 +175,17 @@ def tile_gcrnncell_pb_kernel(
         hc_grouped = {}
         hc_packed = {}
         kept = {}
+
+        def sort(c):
+            nc.vector.tensor_copy(
+                out=hc[c][:, :, :, :, 0 : FEATS // 2]
+                .bitcast(F32)
+                .rearrange("p t b u w -> p (t b) u w"),
+                in_=h_raw[c][:]
+                .rearrange("p t b f -> p (t b f)")
+                .bitcast(F32)
+                .rearrange("p (c w u) -> p c u w", u=2, w=FEATS // 4),
+            )
 
         def diffuse(s):
             c, r = divmod(s, CHUNK_ROUNDS)
@@ -192,10 +210,10 @@ def tile_gcrnncell_pb_kernel(
                         )
             for t in range(PAIR):
                 nc.scalar.copy(
-                    out=hc[c][:, PAIR * r + t, :, FEATS:CHANNELS].rearrange(
-                        "p b (i k) -> p b i k", i=SUPPORTS
+                    out=hc[c][:, PAIR * r + t, :, :, FEATS // 2 : CHANNELS // 2].rearrange(
+                        "p b u (i k) -> p (b u) i k", i=SUPPORTS
                     ),
-                    in_=diffused[t][:].rearrange("p i (b k) -> p b i k", b=BATCH),
+                    in_=diffused[t][:].rearrange("p i (c k) -> p c i k", c=BATCH * 2),
                 )
 
         def flip(s):
@@ -207,7 +225,7 @@ def tile_gcrnncell_pb_kernel(
                     for half in range(2):
                         nc.tensor.transpose(
                             flipped[:, half, t * P : (t + 1) * P],
-                            hc[c][:, PAIR * r + t, b, :].bitcast(F32)[:, half : CHANNELS // 2 : 2],
+                            hc[c][:, PAIR * r + t, b, half, :].bitcast(F32),
                             identity[:],
                         )
                 copy = nc.vector.tensor_copy if b == 0 else nc.scalar.copy
@@ -287,6 +305,8 @@ def tile_gcrnncell_pb_kernel(
             nc.sync.dma_start(out=out_view[s], in_=z[:])
 
         for step in range(ROUNDS + 3):
+            if step % CHUNK_ROUNDS == 1 and step // CHUNK_ROUNDS < CHUNKS:
+                sort(step // CHUNK_ROUNDS)
             if 0 <= step - 2 < ROUNDS:
                 flip(step - 2)
             if 0 <= step - 3 < ROUNDS:

@@ -125,26 +125,26 @@ def tile_gcrnncell_pb_kernel(
             nc.sync.dma_start(out=r_sb[:, :, cols], in_=r_prev.rearrange("b k n -> k b n")[:, :, cols])
         for i in range(SUPPORTS):
             for quad in range(4):
-                nc.sync.dma_start(
-                    out=w_plane[i][32 * quad : 32 * quad + 16, :].bitcast(I32),
-                    in_=support_scales[i][:, 4 * quad : 4 * quad + 4, :].bitcast(I32),
+                nc.gpsimd.dma_start(
+                    out=w_plane[i][32 * quad : 32 * quad + 16, :].bitcast(F32),
+                    in_=support_scales[i][:, 4 * quad : 4 * quad + 4, :].bitcast(F32),
                 )
+        for quad in range(4):
+            nc.gpsimd.dma_start(
+                out=ck_plane[32 * quad : 32 * quad + 4, :].bitcast(F32),
+                in_=c_kernel_scales[0, 4 * quad : 4 * quad + 4, :].bitcast(F32),
+            )
         load_supports(0, CHUNK_ROUNDS)
         ck_words = keep.tile([P, UNITS], U32, align_bytes=64)
+        load_features(0)
+        nc.sync.dma_start(
+            out=ck_words[:].bitcast(I32),
+            in_=c_kernel_words[0].rearrange("p n t -> p (n t)").bitcast(I32),
+        )
         for c in range(CHUNKS):
-            load_features(c)
-            if c == 0:
-                nc.sync.dma_start(
-                    out=ck_words[:].bitcast(I32),
-                    in_=c_kernel_words[0].rearrange("p n t -> p (n t)").bitcast(I32),
-                )
-                for quad in range(4):
-                    nc.sync.dma_start(
-                        out=ck_plane[32 * quad : 32 * quad + 4, :].bitcast(I32),
-                        in_=c_kernel_scales[0, 4 * quad : 4 * quad + 4, :].bitcast(I32),
-                    )
             if c + 1 < CHUNKS:
                 load_supports(c + 1, 1)
+                load_features(c + 1)
             load_gate(c)
         out_view = out.rearrange("b (s x f) -> s x b f", s=ROUNDS, x=P)
 

@@ -80,20 +80,18 @@ def tile_gcrnncell_pb_kernel(
         state_sb = {}
         u_sb = {}
 
-        def load_supports(c, pieces):
-            for i in range(SUPPORTS):
-                w_words[i, c] = keep.tile(
-                    [P, PASSES, CHUNK], U32, name="w_words%d_%d" % (i, c), align_bytes=64
-                )
+        def load_support(i, c, pieces):
+            w_words[i, c] = keep.tile(
+                [P, PASSES, CHUNK], U32, name="w_words%d_%d" % (i, c), align_bytes=64
+            )
             width = CHUNK // pieces
             for piece in range(pieces):
-                for i in range(SUPPORTS):
-                    nc.sync.dma_start(
-                        out=w_words[i, c][:, :, piece * width : (piece + 1) * width].bitcast(I32),
-                        in_=support_words[i]
-                        .rearrange("g p n t -> p g (n t)")
-                        .bitcast(I32)[:, :, c * CHUNK + piece * width : c * CHUNK + (piece + 1) * width],
-                    )
+                nc.sync.dma_start(
+                    out=w_words[i, c][:, :, piece * width : (piece + 1) * width].bitcast(I32),
+                    in_=support_words[i]
+                    .rearrange("g p n t -> p g (n t)")
+                    .bitcast(I32)[:, :, c * CHUNK + piece * width : c * CHUNK + (piece + 1) * width],
+                )
 
         def load_features(c):
             h_raw[c] = keep.tile([P, CHUNK // P, BATCH, FEATS], BF16, name="h_raw%d" % c)
@@ -134,18 +132,20 @@ def tile_gcrnncell_pb_kernel(
                 out=ck_plane[32 * quad : 32 * quad + 4, :].bitcast(F32),
                 in_=c_kernel_scales[0, 4 * quad : 4 * quad + 4, :].bitcast(F32),
             )
-        load_supports(0, CHUNK_ROUNDS)
-        ck_words = keep.tile([P, UNITS], U32, align_bytes=64)
+        load_support(0, 0, 2)
         load_features(0)
+        load_support(1, 0, 1)
+        ck_words = keep.tile([P, UNITS], U32, align_bytes=64)
         nc.sync.dma_start(
             out=ck_words[:].bitcast(I32),
             in_=c_kernel_words[0].rearrange("p n t -> p (n t)").bitcast(I32),
         )
-        for c in range(CHUNKS):
-            if c + 1 < CHUNKS:
-                load_supports(c + 1, 1)
-                load_features(c + 1)
-            load_gate(c)
+        for c in range(1, CHUNKS):
+            load_support(0, c, 1)
+            load_gate(c - 1)
+            load_features(c)
+            load_support(1, c, 2 if c == CHUNKS - 1 else 1)
+        load_gate(CHUNKS - 1)
         out_view = out.rearrange("b (s x f) -> s x b f", s=ROUNDS, x=P)
 
         r_grouped = keep.tile([P, PASSES, BATCH * UNITS, PACK], BF16, align_bytes=64)
@@ -172,9 +172,17 @@ def tile_gcrnncell_pb_kernel(
                 in_=r_grouped[:, g].rearrange("p c t -> p (c t)"),
             )
 
+        banks = {"diffused": 2 * PAIR, "flipped": 2, "prev": 1, "product": 1}
+        diffused = {}
         hc_grouped = {}
         hc_packed = {}
+        prev = {}
         kept = {}
+        product = {}
+        fresh = {}
+        lost = {}
+        z = {}
+        both = slice(0, BATCH)
 
         def sort(c):
             nc.vector.tensor_copy(
@@ -187,40 +195,40 @@ def tile_gcrnncell_pb_kernel(
                 .rearrange("p (c w u) -> p c u w", u=2, w=FEATS // 4),
             )
 
-        def diffuse(s):
-            c, r = divmod(s, CHUNK_ROUNDS)
-            diffused = [
-                psum.tile(
-                    [P, SUPPORTS, BATCH * UNITS], F32, tag="diffused", bufs=2 * PAIR, name="diffused"
+        def diffuse(c, t, i):
+            if i == 0:
+                diffused[c, t] = psum.tile(
+                    [P, SUPPORTS, BATCH * UNITS],
+                    F32,
+                    tag="diffused",
+                    bufs=banks["diffused"],
+                    name="diffused",
                 )
-                for t in range(PAIR)
-            ]
-            for i in range(SUPPORTS):
-                for t in range(PAIR):
-                    first = (PAIR * r + t) * P
-                    for g in range(PASSES):
-                        nc.tensor.matmul_mx(
-                            out=diffused[t][:, i, :],
-                            lhsT=w_words[i, c][:, g, first : first + P].bitcast(FP8X4),
-                            lhsT_scale=w_plane[i][4 * g : P, c * CHUNK + first : c * CHUNK + first + P],
-                            rhs=r_words[:, g, :].bitcast(FP8X4),
-                            rhs_scale=r_plane[:, g, :],
-                            start=(g == 0),
-                            stop=(g == PASSES - 1),
-                        )
-            for t in range(PAIR):
-                nc.scalar.copy(
-                    out=hc[c][:, PAIR * r + t, :, :, FEATS // 2 : CHANNELS // 2].rearrange(
-                        "p b u (i k) -> p (b u) i k", i=SUPPORTS
-                    ),
-                    in_=diffused[t][:].rearrange("p i (c k) -> p c i k", c=BATCH * 2),
+            first = t * P
+            for g in range(PASSES):
+                nc.tensor.matmul_mx(
+                    out=diffused[c, t][:, i, :],
+                    lhsT=w_words[i, c][:, g, first : first + P].bitcast(FP8X4),
+                    lhsT_scale=w_plane[i][4 * g : P, c * CHUNK + first : c * CHUNK + first + P],
+                    rhs=r_words[:, g, :].bitcast(FP8X4),
+                    rhs_scale=r_plane[:, g, :],
+                    start=(g == 0),
+                    stop=(g == PASSES - 1),
                 )
 
-        def flip(s):
+        def settle(c, t):
+            nc.scalar.copy(
+                out=hc[c][:, t, :, :, FEATS // 2 : CHANNELS // 2].rearrange(
+                    "p b u (i k) -> p (b u) i k", i=SUPPORTS
+                ),
+                in_=diffused[c, t][:].rearrange("p i (c k) -> p c i k", c=BATCH * 2),
+            )
+
+        def flip(s, tag):
             c, r = divmod(s, CHUNK_ROUNDS)
             grouped = ring.tile([P, BATCH, PAIR, P, PACK], BF16, align_bytes=64)
             for b in range(BATCH):
-                flipped = psum.tile([P, 2, ROUND], F32, tag="flipped", bufs=2)
+                flipped = psum.tile([P, 2, ROUND], F32, tag=tag, bufs=banks[tag], name="flipped")
                 for t in range(PAIR):
                     for half in range(2):
                         nc.tensor.transpose(
@@ -247,19 +255,22 @@ def tile_gcrnncell_pb_kernel(
                 )
             hc_packed[s] = (hc_words, hc_plane)
 
-        def recall(s):
+        def recall(s, tag):
             c, r = divmod(s, CHUNK_ROUNDS)
-            prev = psum.tile([P, BATCH, UNITS], F32, tag="prev", bufs=1)
+            prev[s] = psum.tile([P, BATCH, UNITS], F32, tag=tag, bufs=banks[tag], name="prev")
             for b in range(BATCH):
                 nc.tensor.transpose(
-                    prev[:, b, :],
+                    prev[s][:, b, :],
                     state_sb[c][:, b, :].bitcast(F32)[:, r * P : (r + 1) * P],
                     identity[:],
                 )
+
+        def hold(s):
+            c, r = divmod(s, CHUNK_ROUNDS)
             kept[s] = ring.tile([P, BATCH, PAIR, UNITS], F32, name="kept")
             nc.vector.tensor_tensor(
                 out=kept[s][:],
-                in0=prev[:]
+                in0=prev[s][:]
                 .rearrange("p b k -> p (b k)")
                 .bitcast(BF16)
                 .rearrange("p (b k j) -> p b j k", b=BATCH, j=PAIR),
@@ -267,14 +278,15 @@ def tile_gcrnncell_pb_kernel(
                 op=alu.mult,
             )
 
-        def candidate(s):
-            c, r = divmod(s, CHUNK_ROUNDS)
+        def multiply(s, tag):
             hc_words, hc_plane = hc_packed[s]
-            product = psum.tile([P, BATCH, PAIR, UNITS], F32, tag="product", bufs=1)
+            product[s] = psum.tile(
+                [P, BATCH, PAIR, UNITS], F32, tag=tag, bufs=banks[tag], name="product"
+            )
             for b in range(BATCH):
                 for j in range(PAIR):
                     nc.tensor.matmul_mx(
-                        out=product[:, b, j, :],
+                        out=product[s][:, b, j, :],
                         lhsT=hc_words[:, b, j, :].bitcast(FP8X4),
                         lhsT_scale=hc_plane[:, b, j, :],
                         rhs=ck_words[:].bitcast(FP8X4),
@@ -282,38 +294,70 @@ def tile_gcrnncell_pb_kernel(
                         start=True,
                         stop=True,
                     )
-            fresh = ring.tile([P, BATCH, PAIR * UNITS], F32)
+            fresh[s] = ring.tile([P, BATCH, PAIR * UNITS], F32, name="fresh")
+            lost[s] = ring.tile([P, BATCH, PAIR * UNITS], F32, name="lost")
+            z[s] = keep.tile([P, BATCH, PAIR * UNITS], F32, name="z%d" % s)
+
+        def squash(s, bs):
             nc.scalar.activation(
-                out=fresh[:], in_=product[:].rearrange("p b j k -> p b (j k)"), func=tanh
+                out=fresh[s][:, bs], in_=product[s][:, bs].rearrange("p b j k -> p b (j k)"), func=tanh
             )
-            lost = ring.tile([P, BATCH, PAIR * UNITS], F32)
+
+        def lose(s, bs):
+            c, r = divmod(s, CHUNK_ROUNDS)
             nc.vector.scalar_tensor_tensor(
-                out=lost[:],
-                in0=u_sb[c][:, r],
+                out=lost[s][:, bs],
+                in0=u_sb[c][:, r, bs],
                 scalar=1.0,
-                in1=fresh[:],
+                in1=fresh[s][:, bs],
                 op0=alu.subtract,
                 op1=alu.mult,
             )
-            z = keep.tile([P, BATCH, PAIR * UNITS], F32, name="z%d" % s)
-            nc.gpsimd.tensor_tensor(
-                out=z[:],
-                in0=kept[s][:].rearrange("p b j k -> p b (j k)"),
-                in1=lost[:],
+
+        def finish(s, bs, engine):
+            engine.tensor_tensor(
+                out=z[s][:, bs],
+                in0=kept[s][:, bs].rearrange("p b j k -> p b (j k)"),
+                in1=lost[s][:, bs],
                 op=alu.subtract,
             )
-            nc.sync.dma_start(out=out_view[s], in_=z[:])
+            nc.sync.dma_start(out=out_view[s][:, bs], in_=z[s][:, bs])
 
-        for step in range(ROUNDS + 3):
-            if step % CHUNK_ROUNDS == 1 and step // CHUNK_ROUNDS < CHUNKS:
-                sort(step // CHUNK_ROUNDS)
-            if 0 <= step - 2 < ROUNDS:
-                flip(step - 2)
-            if 0 <= step - 3 < ROUNDS:
-                recall(step - 3)
-            if 0 <= step - 2 < ROUNDS:
-                pack(step - 2)
-            if 0 <= step - 3 < ROUNDS:
-                candidate(step - 3)
-            if step < ROUNDS:
-                diffuse(step)
+        for step in range(ROUNDS):
+            c, i = divmod(step, SUPPORTS)
+            s = step - 2
+            if s >= 0:
+                flip(s, "flipped")
+                recall(s, "prev")
+                hold(s)
+                pack(s)
+            if i == 0:
+                sort(c)
+            for t in range(CHUNK // P):
+                if s >= 0 and t == CHUNK // P - 1:
+                    multiply(s, "product")
+                    squash(s, both)
+                    lose(s, both)
+                    finish(s, both, nc.gpsimd)
+                diffuse(c, t, i)
+                if i == SUPPORTS - 1:
+                    settle(c, t)
+        last = ROUNDS - 1
+        flip(last - 1, "flipped")
+        flip(last, "diffused")
+        recall(last - 1, "prev")
+        recall(last, "diffused")
+        pack(last - 1)
+        multiply(last - 1, "product")
+        squash(last - 1, both)
+        pack(last)
+        hold(last - 1)
+        multiply(last, "flipped")
+        for b in range(BATCH):
+            squash(last, slice(b, b + 1))
+        lose(last - 1, both)
+        finish(last - 1, both, nc.gpsimd)
+        hold(last)
+        for b in range(BATCH):
+            lose(last, slice(b, b + 1))
+            finish(last, slice(b, b + 1), nc.vector)

@@ -56,13 +56,6 @@ def tile_gcrnncell_pb_kernel(
         ring = ctx.enter_context(tc.tile_pool(name="ring", bufs=2))
         psum = ctx.enter_context(tc.psum_pool(name="psum", bufs=1))
 
-        identity = keep.tile([P, P], F32)
-        make_identity(nc, identity[:])
-        sorter = keep.tile([P, P], F32)
-        nc.vector.tensor_copy(
-            out=sorter[:].rearrange("p (u x e) -> p u x e", u=2, e=2),
-            in_=identity[:].rearrange("p (x u e) -> p u x e", u=2, e=2),
-        )
         w_plane = [
             keep.tile([P, NODES], U8, name="w_plane%d" % i, align_bytes=64) for i in range(SUPPORTS)
         ]
@@ -73,6 +66,13 @@ def tile_gcrnncell_pb_kernel(
         warm = keep.tile([P, 1], F32)
         nc.vector.memset(warm[:], 0.0)
         nc.scalar.activation(out=warm[:], in_=warm[:], func=tanh)
+        identity = keep.tile([P, P], F32)
+        make_identity(nc, identity[:])
+        sorter = keep.tile([P, P], F32)
+        nc.vector.tensor_copy(
+            out=sorter[:].rearrange("p (u x e) -> p u x e", u=2, e=2),
+            in_=identity[:].rearrange("p (x u e) -> p u x e", u=2, e=2),
+        )
 
         w_words = {}
         h_raw = {}
@@ -142,9 +142,9 @@ def tile_gcrnncell_pb_kernel(
         )
         for c in range(1, CHUNKS):
             load_support(0, c, 1)
-            load_gate(c - 1)
             load_features(c)
-            load_support(1, c, 2 if c == CHUNKS - 1 else 1)
+            load_support(1, c, 1)
+            load_gate(c - 1)
         load_gate(CHUNKS - 1)
         out_view = out.rearrange("b (s x f) -> s x b f", s=ROUNDS, x=P)
 
@@ -236,7 +236,7 @@ def tile_gcrnncell_pb_kernel(
                             hc[c][:, PAIR * r + t, b, half, :].bitcast(F32),
                             identity[:],
                         )
-                copy = nc.vector.tensor_copy if b == 0 else nc.scalar.copy
+                copy = nc.vector.tensor_copy if b == 0 and s < ROUNDS - 1 else nc.scalar.copy
                 copy(
                     out=grouped[:, b].bitcast(F32),
                     in_=flipped[:].rearrange("p h (x j) -> p j x h", j=PAIR),
@@ -323,41 +323,28 @@ def tile_gcrnncell_pb_kernel(
             )
             nc.sync.dma_start(out=out_view[s][:, bs], in_=z[s][:, bs])
 
-        for step in range(ROUNDS):
-            c, i = divmod(step, SUPPORTS)
-            s = step - 2
-            if s >= 0:
-                flip(s, "flipped")
+        for step in range(ROUNDS + 3):
+            if 0 <= step - 2 < ROUNDS:
+                flip(step - 2, "flipped")
+            s = step - 3
+            if 0 <= s < ROUNDS:
                 recall(s, "prev")
                 hold(s)
-                pack(s)
-            if i == 0:
-                sort(c)
-            for t in range(CHUNK // P):
-                if s >= 0 and t == CHUNK // P - 1:
-                    multiply(s, "product")
-                    squash(s, both)
-                    lose(s, both)
-                    finish(s, both, nc.gpsimd)
-                diffuse(c, t, i)
-                if i == SUPPORTS - 1:
-                    settle(c, t)
-        last = ROUNDS - 1
-        flip(last - 1, "flipped")
-        flip(last, "diffused")
-        recall(last - 1, "prev")
-        recall(last, "diffused")
-        pack(last - 1)
-        multiply(last - 1, "product")
-        squash(last - 1, both)
-        pack(last)
-        hold(last - 1)
-        multiply(last, "flipped")
-        for b in range(BATCH):
-            squash(last, slice(b, b + 1))
-        lose(last - 1, both)
-        finish(last - 1, both, nc.gpsimd)
-        hold(last)
-        for b in range(BATCH):
-            lose(last, slice(b, b + 1))
-            finish(last, slice(b, b + 1), nc.vector)
+            if 0 <= step - 2 < ROUNDS:
+                pack(step - 2)
+            if 0 <= s < ROUNDS:
+                multiply(s, "product")
+                parts = [slice(b, b + 1) for b in range(BATCH)] if s == ROUNDS - 1 else [both]
+                for bs in parts:
+                    squash(s, bs)
+                for bs in parts:
+                    lose(s, bs)
+                    finish(s, bs, nc.vector if s >= ROUNDS - 3 else nc.gpsimd)
+            if step < ROUNDS:
+                c, i = divmod(step, SUPPORTS)
+                if i == 0:
+                    sort(c)
+                for t in range(CHUNK // P):
+                    diffuse(c, t, i)
+                    if i == SUPPORTS - 1:
+                        settle(c, t)

@@ -102,12 +102,14 @@ def tile_gcrnncell_pb_kernel(
                     in_=h_diff[b, c * CHUNK : (c + 1) * CHUNK, :].rearrange("(t x) f -> x t f", x=P),
                 )
 
-        def load_gate(c):
+        def load_state(c):
             state_sb[c] = keep.tile([P, BATCH, CHUNK], BF16, name="state%d" % c)
             nc.sync.dma_start(
                 out=state_sb[c][:],
                 in_=state.rearrange("b (k n) -> k b n", n=NODES)[:, :, c * CHUNK : (c + 1) * CHUNK],
             )
+
+        def load_update(c):
             u_sb[c] = keep.tile([P, CHUNK_ROUNDS, BATCH, PAIR * UNITS], BF16, name="u%d" % c)
             for b in range(BATCH):
                 nc.sync.dma_start(
@@ -143,9 +145,11 @@ def tile_gcrnncell_pb_kernel(
         for c in range(1, CHUNKS):
             load_support(0, c, 1)
             load_features(c)
+            load_state(c - 1)
             load_support(1, c, 1)
-            load_gate(c - 1)
-        load_gate(CHUNKS - 1)
+            load_update(c - 1)
+        load_state(CHUNKS - 1)
+        load_update(CHUNKS - 1)
         out_view = out.rearrange("b (s x f) -> s x b f", s=ROUNDS, x=P)
 
         r_grouped = keep.tile([P, PASSES, BATCH * UNITS, PACK], BF16, align_bytes=64)

@@ -22,10 +22,11 @@ CHANNELS = FEATS + SUPPORTS * UNITS
 PASSES = NODES // K_PASS
 CHUNK = 512
 CHUNKS = NODES // CHUNK
+TILES = CHUNK // P
 PAIR = 2
+PAIRS = TILES // PAIR
 ROUND = PAIR * P
 ROUNDS = NODES // ROUND
-CHUNK_ROUNDS = CHUNK // ROUND
 
 FLOPS = 2 * BATCH * UNITS * NODES * NODES * SUPPORTS + 2 * BATCH * NODES * CHANNELS * UNITS
 
@@ -59,9 +60,10 @@ def tile_gcrnncell_pb_kernel(
         w_plane = [
             keep.tile([P, NODES], U8, name="w_plane%d" % i, align_bytes=64) for i in range(SUPPORTS)
         ]
-        ck_plane = keep.tile([P, UNITS], U8, align_bytes=64)
         for i in range(SUPPORTS):
             nc.vector.memset(w_plane[i][:].bitcast(I32), 0)
+        ck_words = keep.tile([P, UNITS], U32, align_bytes=64)
+        ck_plane = keep.tile([P, UNITS], U8, align_bytes=64)
         nc.vector.memset(ck_plane[:].bitcast(I32), 0)
         warm = keep.tile([P, 1], F32)
         nc.vector.memset(warm[:], 0.0)
@@ -70,93 +72,123 @@ def tile_gcrnncell_pb_kernel(
         make_identity(nc, identity[:])
         sorter = keep.tile([P, P], F32)
         nc.vector.tensor_copy(
-            out=sorter[:].rearrange("p (u x e) -> p u x e", u=2, e=2),
-            in_=identity[:].rearrange("p (x u e) -> p u x e", u=2, e=2),
+            out=sorter[:].rearrange("p (v x e) -> p v x e", v=2, e=2),
+            in_=identity[:].rearrange("p (x v e) -> p v x e", v=2, e=2),
         )
 
         w_words = {}
-        h_raw = {}
         hc = {}
+        h_raw = {}
         state_sb = {}
         u_sb = {}
 
-        def load_support(i, c, pieces):
-            w_words[i, c] = keep.tile(
-                [P, PASSES, CHUNK], U32, name="w_words%d_%d" % (i, c), align_bytes=64
+        def load_support(i, rounds):
+            words = keep.tile(
+                [P, PASSES, len(rounds) * ROUND],
+                U32,
+                name="w_words%d_%d" % (i, rounds[0]),
+                align_bytes=64,
             )
-            width = CHUNK // pieces
-            for piece in range(pieces):
-                nc.sync.dma_start(
-                    out=w_words[i, c][:, :, piece * width : (piece + 1) * width].bitcast(I32),
-                    in_=support_words[i]
-                    .rearrange("g p n t -> p g (n t)")
-                    .bitcast(I32)[:, :, c * CHUNK + piece * width : c * CHUNK + (piece + 1) * width],
-                )
-
-        def load_features(c):
-            h_raw[c] = keep.tile([P, CHUNK // P, BATCH, FEATS], BF16, name="h_raw%d" % c)
-            hc[c] = keep.tile([P, CHUNK // P, BATCH, 2, CHANNELS // 2], BF16, name="hc%d" % c)
-            for b in range(BATCH):
-                nc.sync.dma_start(
-                    out=h_raw[c][:, :, b, :],
-                    in_=h_diff[b, c * CHUNK : (c + 1) * CHUNK, :].rearrange("(t x) f -> x t f", x=P),
-                )
-
-        def load_state(c):
-            state_sb[c] = keep.tile([P, BATCH, CHUNK], BF16, name="state%d" % c)
             nc.sync.dma_start(
-                out=state_sb[c][:],
-                in_=state.rearrange("b (k n) -> k b n", n=NODES)[:, :, c * CHUNK : (c + 1) * CHUNK],
+                out=words[:].bitcast(I32),
+                in_=support_words[i]
+                .rearrange("g p n t -> p g (n t)")
+                .bitcast(I32)[:, :, rounds[0] * ROUND : (rounds[-1] + 1) * ROUND],
             )
+            for n, s in enumerate(rounds):
+                w_words[i, s] = words[:, :, n * ROUND : (n + 1) * ROUND]
 
-        def load_update(c):
-            u_sb[c] = keep.tile([P, CHUNK_ROUNDS, BATCH, PAIR * UNITS], BF16, name="u%d" % c)
+        def load_features(rounds):
+            for s in rounds:
+                hc[s] = keep.tile([P, PAIR, BATCH, 2, CHANNELS // 2], BF16, name="hc%d" % s)
+            raw = keep.tile(
+                [P, PAIR * len(rounds), BATCH, FEATS], BF16, name="h_raw%d" % rounds[0]
+            )
             for b in range(BATCH):
                 nc.sync.dma_start(
-                    out=u_sb[c][:, :, b, :],
-                    in_=u[b, c * CHUNK : (c + 1) * CHUNK, :].rearrange(
+                    out=raw[:, :, b, :],
+                    in_=h_diff[b, rounds[0] * ROUND : (rounds[-1] + 1) * ROUND, :].rearrange(
+                        "(t x) f -> x t f", x=P
+                    ),
+                )
+            for n, s in enumerate(rounds):
+                h_raw[s] = raw[:, PAIR * n : PAIR * (n + 1)]
+
+        def load_state(rounds):
+            tile = keep.tile([P, BATCH, len(rounds) * ROUND], BF16, name="state%d" % rounds[0])
+            nc.sync.dma_start(
+                out=tile[:],
+                in_=state.rearrange("b (k n) -> k b n", n=NODES)[
+                    :, :, rounds[0] * ROUND : (rounds[-1] + 1) * ROUND
+                ],
+            )
+            for n, s in enumerate(rounds):
+                state_sb[s] = tile[:, :, n * ROUND : (n + 1) * ROUND]
+
+        def load_update(rounds):
+            tile = keep.tile(
+                [P, len(rounds), BATCH, PAIR * UNITS], BF16, name="u%d" % rounds[0]
+            )
+            for b in range(BATCH):
+                nc.sync.dma_start(
+                    out=tile[:, :, b, :],
+                    in_=u[b, rounds[0] * ROUND : (rounds[-1] + 1) * ROUND, :].rearrange(
                         "(r x j) k -> x r (j k)", x=P, j=PAIR
                     ),
                 )
+            for n, s in enumerate(rounds):
+                u_sb[s] = tile[:, n]
 
         r_sb = keep.tile([P, BATCH, NODES], BF16)
         for part in range(2):
             cols = slice(part * NODES // 2, (part + 1) * NODES // 2)
             nc.sync.dma_start(out=r_sb[:, :, cols], in_=r_prev.rearrange("b k n -> k b n")[:, :, cols])
         for i in range(SUPPORTS):
-            for quad in range(4):
+            for quadrant in range(4):
                 nc.gpsimd.dma_start(
-                    out=w_plane[i][32 * quad : 32 * quad + 16, :].bitcast(F32),
-                    in_=support_scales[i][:, 4 * quad : 4 * quad + 4, :].bitcast(F32),
+                    out=w_plane[i][32 * quadrant : 32 * quadrant + 16, :].bitcast(F32),
+                    in_=support_scales[i][:, 4 * quadrant : 4 * quadrant + 4, :].bitcast(F32),
                 )
-        for quad in range(4):
+        for quadrant in range(4):
             nc.gpsimd.dma_start(
-                out=ck_plane[32 * quad : 32 * quad + 4, :].bitcast(F32),
-                in_=c_kernel_scales[0, 4 * quad : 4 * quad + 4, :].bitcast(F32),
+                out=ck_plane[32 * quadrant : 32 * quadrant + 4, :].bitcast(F32),
+                in_=c_kernel_scales[0, 4 * quadrant : 4 * quadrant + 4, :].bitcast(F32),
             )
-        load_support(0, 0, 2)
-        load_features(0)
-        load_support(1, 0, 1)
-        ck_words = keep.tile([P, UNITS], U32, align_bytes=64)
+        G = [[0, 1], [2, 3], [4, 5], [6, 7]]
+        load_support(0, [0])
+        load_support(0, [1])
+        load_features([0, 1])
+        load_support(1, [0, 1])
         nc.sync.dma_start(
             out=ck_words[:].bitcast(I32),
             in_=c_kernel_words[0].rearrange("p n t -> p (n t)").bitcast(I32),
         )
-        for c in range(1, CHUNKS):
-            load_support(0, c, 1)
-            load_features(c)
-            load_state(c - 1)
-            load_support(1, c, 1)
-            load_update(c - 1)
-        load_state(CHUNKS - 1)
-        load_update(CHUNKS - 1)
-        out_view = out.rearrange("b (s x f) -> s x b f", s=ROUNDS, x=P)
+        for c in range(1, 4):
+            if c < 3:
+                load_support(0, [2 * c, 2 * c + 1])
+                load_features([2 * c, 2 * c + 1])
+                load_state([2 * c - 2, 2 * c - 1])
+                load_support(1, [2 * c, 2 * c + 1])
+                load_update([2 * c - 2, 2 * c - 1])
+            else:
+                load_support(0, [6, 7])
+                load_features([6, 7])
+                load_state([4, 5])
+                load_support(1, [6])
+                load_update([4, 5])
+                load_support(1, [7])
+                load_state([6, 7])
+                load_update([6, 7])
+        banks = {"diffused": 2, "flipped": 3, "prev": 1, "product": 2}
 
         r_grouped = keep.tile([P, PASSES, BATCH * UNITS, PACK], BF16, align_bytes=64)
         r_words = keep.tile([P, PASSES, BATCH * UNITS], U32, align_bytes=64)
         r_plane = keep.tile([P, PASSES, BATCH * UNITS], U8, align_bytes=64)
-        for g in range(PASSES):
-            r_flipped = psum.tile([P, 2, BATCH, UNITS], F32, tag="diffused", bufs=2 * PAIR)
+
+        def r_flip(g):
+            r_flipped = psum.tile(
+                [P, 2, BATCH, UNITS], F32, tag="flipped", bufs=banks["flipped"], name="r_flipped"
+            )
             for b in range(BATCH):
                 for half in range(2):
                     nc.tensor.transpose(
@@ -165,142 +197,132 @@ def tile_gcrnncell_pb_kernel(
                         sorter[:],
                     )
             copy = nc.vector.tensor_copy if g % 2 == 0 else nc.scalar.copy
-            copy(
-                out=r_grouped[:, g].bitcast(F32),
-                in_=r_flipped[:].rearrange("p h b k -> p (b k) h"),
-            )
-        for g in range(PASSES):
+            copy(out=r_grouped[:, g].bitcast(F32), in_=r_flipped[:].rearrange("p h b k -> p (b k) h"))
+
+        def r_pack(g):
             nc.vector.quantize_mx(
                 out=r_words[:, g, :].bitcast(FP8X4),
                 scales=r_plane[:, g, :],
                 in_=r_grouped[:, g].rearrange("p c t -> p (c t)"),
             )
 
-        banks = {"diffused": 2 * PAIR, "flipped": 2, "prev": 1, "product": 1}
-        diffused = {}
         hc_grouped = {}
         hc_packed = {}
+        diffused = {}
         prev = {}
         kept = {}
         product = {}
         fresh = {}
         lost = {}
         z = {}
-        both = slice(0, BATCH)
 
-        def sort(c):
+        def sort(s):
             nc.vector.tensor_copy(
-                out=hc[c][:, :, :, :, 0 : FEATS // 2]
-                .bitcast(F32)
-                .rearrange("p t b u w -> p (t b) u w"),
-                in_=h_raw[c][:]
+                out=hc[s][:, :, :, :, 0 : FEATS // 2].bitcast(F32).rearrange("p t b v w -> p (t b) v w"),
+                in_=h_raw[s]
                 .rearrange("p t b f -> p (t b f)")
                 .bitcast(F32)
-                .rearrange("p (c w u) -> p c u w", u=2, w=FEATS // 4),
+                .rearrange("p (c w v) -> p c v w", v=2, w=FEATS // 4),
             )
 
-        def diffuse(c, t, i):
-            if i == 0:
-                diffused[c, t] = psum.tile(
-                    [P, SUPPORTS, BATCH * UNITS],
-                    F32,
-                    tag="diffused",
-                    bufs=banks["diffused"],
-                    name="diffused",
-                )
-            first = t * P
-            for g in range(PASSES):
-                nc.tensor.matmul_mx(
-                    out=diffused[c, t][:, i, :],
-                    lhsT=w_words[i, c][:, g, first : first + P].bitcast(FP8X4),
-                    lhsT_scale=w_plane[i][4 * g : P, c * CHUNK + first : c * CHUNK + first + P],
-                    rhs=r_words[:, g, :].bitcast(FP8X4),
-                    rhs_scale=r_plane[:, g, :],
-                    start=(g == 0),
-                    stop=(g == PASSES - 1),
-                )
-
-        def settle(c, t):
-            nc.scalar.copy(
-                out=hc[c][:, t, :, :, FEATS // 2 : CHANNELS // 2].rearrange(
-                    "p b u (i k) -> p (b u) i k", i=SUPPORTS
-                ),
-                in_=diffused[c, t][:].rearrange("p i (c k) -> p c i k", c=BATCH * 2),
+        def diffuse(i, s):
+            diffused[i, s] = psum.tile(
+                [P, PAIR, BATCH * UNITS], F32, tag="diffused", bufs=banks["diffused"], name="diffused"
             )
+            for t in range(PAIR):
+                first = t * P
+                for g in range(PASSES):
+                    nc.tensor.matmul_mx(
+                        out=diffused[i, s][:, t, :],
+                        lhsT=w_words[i, s][:, g, first : first + P].bitcast(FP8X4),
+                        lhsT_scale=w_plane[i][4 * g : P, s * ROUND + first : s * ROUND + first + P],
+                        rhs=r_words[:, g, :].bitcast(FP8X4),
+                        rhs_scale=r_plane[:, g, :],
+                        start=(g == 0),
+                        stop=(g == PASSES - 1),
+                    )
 
-        def flip(s, tag):
-            c, r = divmod(s, CHUNK_ROUNDS)
-            grouped = ring.tile([P, BATCH, PAIR, P, PACK], BF16, align_bytes=64)
+        def settle(i, s, engines):
+            first = FEATS // 2 + i * UNITS // 2
+            for n, engine in enumerate(engines):
+                ts = slice(n * PAIR // len(engines), (n + 1) * PAIR // len(engines))
+                engine(
+                    out=hc[s][:, ts, :, :, first : first + UNITS // 2].rearrange(
+                        "p t b v k -> p (t b v) k"
+                    ),
+                    in_=diffused[i, s][:, ts].rearrange("p t (c k) -> p (t c) k", k=UNITS // 2),
+                )
+
+        def flip(s, engines):
+            grouped = ring.tile([P, BATCH, PAIR, P, PACK], BF16, align_bytes=64, name="hc_grouped")
             for b in range(BATCH):
-                flipped = psum.tile([P, 2, ROUND], F32, tag=tag, bufs=banks[tag], name="flipped")
+                flipped = psum.tile([P, 2, ROUND], F32, tag="flipped", bufs=banks["flipped"], name="flipped")
                 for t in range(PAIR):
                     for half in range(2):
                         nc.tensor.transpose(
                             flipped[:, half, t * P : (t + 1) * P],
-                            hc[c][:, PAIR * r + t, b, half, :].bitcast(F32),
+                            hc[s][:, t, b, half, :].bitcast(F32),
                             identity[:],
                         )
-                copy = nc.vector.tensor_copy if b == 0 and s < ROUNDS - 1 else nc.scalar.copy
-                copy(
+                engines[b](
                     out=grouped[:, b].bitcast(F32),
                     in_=flipped[:].rearrange("p h (x j) -> p j x h", j=PAIR),
                 )
             hc_grouped[s] = grouped
+            hc_packed[s] = (
+                ring.tile([P, BATCH, PAIR, P], U32, align_bytes=64, name="hc_words"),
+                ring.tile([P, BATCH, PAIR, P], U8, align_bytes=64, name="hc_plane"),
+            )
 
         def pack(s):
-            grouped = hc_grouped[s]
-            hc_words = ring.tile([P, BATCH, PAIR, P], U32, align_bytes=64)
-            hc_plane = ring.tile([P, BATCH, PAIR, P], U8, align_bytes=64)
+            words, plane = hc_packed[s]
             for b in range(BATCH):
                 nc.vector.quantize_mx(
-                    out=hc_words[:, b].rearrange("p j x -> p (j x)").bitcast(FP8X4),
-                    scales=hc_plane[:, b].rearrange("p j x -> p (j x)"),
-                    in_=grouped[:, b].rearrange("p j x t -> p (j x t)"),
+                    out=words[:, b].rearrange("p j x -> p (j x)").bitcast(FP8X4),
+                    scales=plane[:, b].rearrange("p j x -> p (j x)"),
+                    in_=hc_grouped[s][:, b].rearrange("p j x t -> p (j x t)"),
                 )
-            hc_packed[s] = (hc_words, hc_plane)
 
-        def recall(s, tag):
-            c, r = divmod(s, CHUNK_ROUNDS)
-            prev[s] = psum.tile([P, BATCH, UNITS], F32, tag=tag, bufs=banks[tag], name="prev")
-            for b in range(BATCH):
-                nc.tensor.transpose(
-                    prev[s][:, b, :],
-                    state_sb[c][:, b, :].bitcast(F32)[:, r * P : (r + 1) * P],
-                    identity[:],
-                )
+        def recall(rounds):
+            tile = psum.tile([P, 2, BATCH, UNITS], F32, tag="prev", bufs=banks["prev"], name="prev")
+            for n, s in enumerate(rounds):
+                prev[s] = tile[:, n]
+                for b in range(BATCH):
+                    nc.tensor.transpose(
+                        tile[:, n, b, :],
+                        state_sb[s][:, b, :].bitcast(F32),
+                        identity[:],
+                    )
 
         def hold(s):
-            c, r = divmod(s, CHUNK_ROUNDS)
-            kept[s] = ring.tile([P, BATCH, PAIR, UNITS], F32, name="kept")
+            kept[s] = ring.tile([P, BATCH, PAIR, UNITS], F32, name="kept", bufs=3)
             nc.vector.tensor_tensor(
                 out=kept[s][:],
-                in0=prev[s][:]
+                in0=prev[s]
                 .rearrange("p b k -> p (b k)")
                 .bitcast(BF16)
                 .rearrange("p (b k j) -> p b j k", b=BATCH, j=PAIR),
-                in1=u_sb[c][:, r].rearrange("p b (j k) -> p b j k", j=PAIR),
+                in1=u_sb[s].rearrange("p b (j k) -> p b j k", j=PAIR),
                 op=alu.mult,
             )
 
-        def multiply(s, tag):
-            hc_words, hc_plane = hc_packed[s]
-            product[s] = psum.tile(
-                [P, BATCH, PAIR, UNITS], F32, tag=tag, bufs=banks[tag], name="product"
-            )
+        def multiply(s):
+            product[s] = psum.tile([P, BATCH, PAIR, UNITS], F32, tag="product", bufs=banks["product"], name="product")
+            words, plane = hc_packed[s]
+            fresh[s] = ring.tile([P, BATCH, PAIR * UNITS], F32, name="fresh")
+            lost[s] = ring.tile([P, BATCH, PAIR * UNITS], F32, name="lost")
+            z[s] = keep.tile([P, BATCH, PAIR * UNITS], F32, name="z%d" % s)
             for b in range(BATCH):
                 for j in range(PAIR):
                     nc.tensor.matmul_mx(
                         out=product[s][:, b, j, :],
-                        lhsT=hc_words[:, b, j, :].bitcast(FP8X4),
-                        lhsT_scale=hc_plane[:, b, j, :],
+                        lhsT=words[:, b, j, :].bitcast(FP8X4),
+                        lhsT_scale=plane[:, b, j, :],
                         rhs=ck_words[:].bitcast(FP8X4),
                         rhs_scale=ck_plane[:],
                         start=True,
                         stop=True,
                     )
-            fresh[s] = ring.tile([P, BATCH, PAIR * UNITS], F32, name="fresh")
-            lost[s] = ring.tile([P, BATCH, PAIR * UNITS], F32, name="lost")
-            z[s] = keep.tile([P, BATCH, PAIR * UNITS], F32, name="z%d" % s)
 
         def squash(s, bs):
             nc.scalar.activation(
@@ -308,15 +330,16 @@ def tile_gcrnncell_pb_kernel(
             )
 
         def lose(s, bs):
-            c, r = divmod(s, CHUNK_ROUNDS)
             nc.vector.scalar_tensor_tensor(
                 out=lost[s][:, bs],
-                in0=u_sb[c][:, r, bs],
+                in0=u_sb[s][:, bs],
                 scalar=1.0,
                 in1=fresh[s][:, bs],
                 op0=alu.subtract,
                 op1=alu.mult,
             )
+
+        out_view = out.rearrange("b (s x f) -> s x b f", s=ROUNDS, x=P)
 
         def finish(s, bs, engine):
             engine.tensor_tensor(
@@ -327,28 +350,48 @@ def tile_gcrnncell_pb_kernel(
             )
             nc.sync.dma_start(out=out_view[s][:, bs], in_=z[s][:, bs])
 
-        for step in range(ROUNDS + 3):
-            if 0 <= step - 2 < ROUNDS:
-                flip(step - 2, "flipped")
-            s = step - 3
-            if 0 <= s < ROUNDS:
-                recall(s, "prev")
-                hold(s)
-            if 0 <= step - 2 < ROUNDS:
-                pack(step - 2)
-            if 0 <= s < ROUNDS:
-                multiply(s, "product")
-                parts = [slice(b, b + 1) for b in range(BATCH)] if s == ROUNDS - 1 else [both]
-                for bs in parts:
-                    squash(s, bs)
-                for bs in parts:
-                    lose(s, bs)
-                    finish(s, bs, nc.vector if s >= ROUNDS - 3 else nc.gpsimd)
-            if step < ROUNDS:
-                c, i = divmod(step, SUPPORTS)
-                if i == 0:
-                    sort(c)
-                for t in range(CHUNK // P):
-                    diffuse(c, t, i)
-                    if i == SUPPORTS - 1:
-                        settle(c, t)
+        for g in range(PASSES):
+            r_flip(g)
+            if g % 2 == 1:
+                r_pack(g - 1)
+                r_pack(g)
+        V, S = nc.vector.tensor_copy, nc.scalar.copy
+        both = slice(0, BATCH)
+        single = [slice(b, b + 1) for b in range(BATCH)]
+        gp, ve = nc.gpsimd, nc.vector
+        slots = [(i, s) for group in [[0, 1], [2, 3], [4, 5], [6, 7]] for i in range(SUPPORTS) for s in group]
+        done = {s: n for n, (i, s) in enumerate(slots) if i == SUPPORTS - 1}
+        whole = {s: done[group[-1]] for group in [[0, 1], [2, 3], [4, 5], [6, 7]] for s in group}
+        def parts(s):
+            return single if s >= 6 else [both]
+        for n in range(len(slots) + 5):
+            if n < len(slots):
+                diffuse(*slots[n])
+                settle(*slots[n], (S,))
+            for s in range(ROUNDS):
+                if n == done[s] - 2:
+                    sort(s)
+                if n == done[s] + 1:
+                    flip(s, (S, S) if s == ROUNDS - 1 else (S, S))
+                    for group in [[0, 1], [2, 3], [4, 5], [6, 7]]:
+                        if s == group[-1]:
+                            recall(group)
+            for s in range(ROUNDS):
+                if n == done[s] + 1:
+                    pack(s)
+            for s in range(ROUNDS):
+                if n == done[s] + 2:
+                    multiply(s)
+                    for bs in parts(s):
+                        squash(s, bs)
+            for s in range(ROUNDS):
+                if n == whole[s] + 2:
+                    hold(s)
+            for s in range(ROUNDS):
+                if n == max(done[s] + 2, whole[s] + 2) + 1:
+                    for bs in parts(s):
+                        finish(s, bs, ve if s >= 0 else gp)
+            for s in range(ROUNDS):
+                if n == done[s] + 2:
+                    for bs in parts(s):
+                        lose(s, bs)

@@ -58,12 +58,12 @@ def tile_gcrnncell_pb_kernel(
         psum = ctx.enter_context(tc.psum_pool(name="psum", bufs=1))
 
         w_plane = [
-            keep.tile([P, NODES], U8, name="w_plane%d" % i, align_bytes=64) for i in range(SUPPORTS)
+            keep.tile([P, NODES], U8, name="w_plane%d" % i, align_bytes=256) for i in range(SUPPORTS)
         ]
         for i in range(SUPPORTS):
             nc.vector.memset(w_plane[i][:].bitcast(I32), 0)
-        ck_words = keep.tile([P, UNITS], U32, align_bytes=64)
-        ck_plane = keep.tile([P, UNITS], U8, align_bytes=64)
+        ck_words = keep.tile([P, UNITS], U32, align_bytes=256)
+        ck_plane = keep.tile([P, UNITS], U8, align_bytes=256)
         nc.vector.memset(ck_plane[:].bitcast(I32), 0)
         warm = keep.tile([P, 1], F32)
         nc.vector.memset(warm[:], 0.0)
@@ -87,7 +87,7 @@ def tile_gcrnncell_pb_kernel(
                 [P, PASSES, len(rounds) * ROUND],
                 U32,
                 name="w_words%d_%d" % (i, rounds[0]),
-                align_bytes=64,
+                align_bytes=256,
             )
             nc.sync.dma_start(
                 out=words[:].bitcast(I32),
@@ -181,9 +181,9 @@ def tile_gcrnncell_pb_kernel(
                 load_update([6, 7])
         banks = {"diffused": 2, "flipped": 3, "prev": 1, "product": 2}
 
-        r_grouped = keep.tile([P, PASSES, BATCH * UNITS, PACK], BF16, align_bytes=64)
-        r_words = keep.tile([P, PASSES, BATCH * UNITS], U32, align_bytes=64)
-        r_plane = keep.tile([P, PASSES, BATCH * UNITS], U8, align_bytes=64)
+        r_grouped = keep.tile([P, PASSES, BATCH * UNITS, PACK], BF16, align_bytes=256)
+        r_words = keep.tile([P, PASSES, BATCH * UNITS], U32, align_bytes=256)
+        r_plane = keep.tile([P, PASSES, BATCH * UNITS], U8, align_bytes=256)
 
         def r_flip(g):
             r_flipped = psum.tile(
@@ -254,7 +254,7 @@ def tile_gcrnncell_pb_kernel(
                 )
 
         def flip(s, engines):
-            grouped = ring.tile([P, BATCH, PAIR, P, PACK], BF16, align_bytes=64, name="hc_grouped")
+            grouped = ring.tile([P, BATCH, PAIR, P, PACK], BF16, align_bytes=256, name="hc_grouped")
             for b in range(BATCH):
                 flipped = psum.tile([P, 2, ROUND], F32, tag="flipped", bufs=banks["flipped"], name="flipped")
                 for t in range(PAIR):
@@ -270,8 +270,8 @@ def tile_gcrnncell_pb_kernel(
                 )
             hc_grouped[s] = grouped
             hc_packed[s] = (
-                ring.tile([P, BATCH, PAIR, P], U32, align_bytes=64, name="hc_words"),
-                ring.tile([P, BATCH, PAIR, P], U8, align_bytes=64, name="hc_plane"),
+                ring.tile([P, BATCH, PAIR, P], U32, align_bytes=256, name="hc_words"),
+                ring.tile([P, BATCH, PAIR, P], U8, align_bytes=256, name="hc_plane"),
             )
 
         def pack(s):

@@ -65,12 +65,12 @@ def tile_gcrnncell_pb_kernel(
         ck_words = keep.tile([P, UNITS], U32, align_bytes=256)
         ck_plane = keep.tile([P, UNITS], U8, align_bytes=256)
         nc.vector.memset(ck_plane[:].bitcast(I32), 0)
-        warm = keep.tile([P, 1], F32)
+        warm = keep.tile([P, 1], F32, align_bytes=256)
         nc.vector.memset(warm[:], 0.0)
         nc.scalar.activation(out=warm[:], in_=warm[:], func=tanh)
-        identity = keep.tile([P, P], F32)
+        identity = keep.tile([P, P], F32, align_bytes=256)
         make_identity(nc, identity[:])
-        sorter = keep.tile([P, P], F32)
+        sorter = keep.tile([P, P], F32, align_bytes=256)
         nc.vector.tensor_copy(
             out=sorter[:].rearrange("p (v x e) -> p v x e", v=2, e=2),
             in_=identity[:].rearrange("p (x v e) -> p v x e", v=2, e=2),
@@ -100,10 +100,9 @@ def tile_gcrnncell_pb_kernel(
 
         def load_features(rounds):
             for s in rounds:
-                hc[s] = keep.tile([P, PAIR, BATCH, 2, CHANNELS // 2], BF16, name="hc%d" % s)
+                hc[s] = keep.tile([P, PAIR, BATCH, 2, CHANNELS // 2], BF16, name="hc%d" % s, align_bytes=256)
             raw = keep.tile(
-                [P, PAIR * len(rounds), BATCH, FEATS], BF16, name="h_raw%d" % rounds[0]
-            )
+                [P, PAIR * len(rounds), BATCH, FEATS], BF16, name="h_raw%d" % rounds[0], align_bytes=256)
             for b in range(BATCH):
                 nc.sync.dma_start(
                     out=raw[:, :, b, :],
@@ -115,7 +114,7 @@ def tile_gcrnncell_pb_kernel(
                 h_raw[s] = raw[:, PAIR * n : PAIR * (n + 1)]
 
         def load_state(rounds):
-            tile = keep.tile([P, BATCH, len(rounds) * ROUND], BF16, name="state%d" % rounds[0])
+            tile = keep.tile([P, BATCH, len(rounds) * ROUND], BF16, name="state%d" % rounds[0], align_bytes=256)
             nc.sync.dma_start(
                 out=tile[:],
                 in_=state.rearrange("b (k n) -> k b n", n=NODES)[
@@ -127,8 +126,7 @@ def tile_gcrnncell_pb_kernel(
 
         def load_update(rounds):
             tile = keep.tile(
-                [P, len(rounds), BATCH, PAIR * UNITS], BF16, name="u%d" % rounds[0]
-            )
+                [P, len(rounds), BATCH, PAIR * UNITS], BF16, name="u%d" % rounds[0], align_bytes=256)
             for b in range(BATCH):
                 nc.sync.dma_start(
                     out=tile[:, :, b, :],
@@ -139,7 +137,7 @@ def tile_gcrnncell_pb_kernel(
             for n, s in enumerate(rounds):
                 u_sb[s] = tile[:, n]
 
-        r_sb = keep.tile([P, BATCH, NODES], BF16)
+        r_sb = keep.tile([P, BATCH, NODES], BF16, align_bytes=256)
         for part in range(2):
             cols = slice(part * NODES // 2, (part + 1) * NODES // 2)
             nc.sync.dma_start(out=r_sb[:, :, cols], in_=r_prev.rearrange("b k n -> k b n")[:, :, cols])
@@ -216,8 +214,8 @@ def tile_gcrnncell_pb_kernel(
         lost = {}
         z = {}
 
-        def sort(s):
-            nc.vector.tensor_copy(
+        def sort(s, engine=nc.vector.tensor_copy):
+            engine(
                 out=hc[s][:, :, :, :, 0 : FEATS // 2].bitcast(F32).rearrange("p t b v w -> p (t b) v w"),
                 in_=h_raw[s]
                 .rearrange("p t b f -> p (t b f)")
@@ -295,7 +293,7 @@ def tile_gcrnncell_pb_kernel(
                     )
 
         def hold(s):
-            kept[s] = ring.tile([P, BATCH, PAIR, UNITS], F32, name="kept", bufs=3)
+            kept[s] = ring.tile([P, BATCH, PAIR, UNITS], F32, name="kept", bufs=3, align_bytes=256)
             nc.vector.tensor_tensor(
                 out=kept[s][:],
                 in0=prev[s]
@@ -309,9 +307,9 @@ def tile_gcrnncell_pb_kernel(
         def multiply(s):
             product[s] = psum.tile([P, BATCH, PAIR, UNITS], F32, tag="product", bufs=banks["product"], name="product")
             words, plane = hc_packed[s]
-            fresh[s] = ring.tile([P, BATCH, PAIR * UNITS], F32, name="fresh")
-            lost[s] = ring.tile([P, BATCH, PAIR * UNITS], F32, name="lost")
-            z[s] = keep.tile([P, BATCH, PAIR * UNITS], F32, name="z%d" % s)
+            fresh[s] = ring.tile([P, BATCH, PAIR * UNITS], F32, name="fresh", align_bytes=256)
+            lost[s] = ring.tile([P, BATCH, PAIR * UNITS], F32, name="lost", align_bytes=256)
+            z[s] = keep.tile([P, BATCH, PAIR * UNITS], F32, name="z%d" % s, align_bytes=256)
             for b in range(BATCH):
                 for j in range(PAIR):
                     nc.tensor.matmul_mx(
@@ -369,29 +367,33 @@ def tile_gcrnncell_pb_kernel(
                 diffuse(*slots[n])
                 settle(*slots[n], (S,))
             for s in range(ROUNDS):
-                if n == done[s] - 2:
-                    sort(s)
-                if n == done[s] + 1:
-                    flip(s, (S, S) if s == ROUNDS - 1 else (S, S))
-                    for group in [[0, 1], [2, 3], [4, 5], [6, 7]]:
-                        if s == group[-1]:
-                            recall(group)
+                if n == done[s] - (-1 if s >= 9 else 2):
+                    sort(s, S if s >= 9 and False else V)
+            if n == done[ROUNDS - 1] + 1:
+                recall([6, 7])
             for s in range(ROUNDS):
-                if n == done[s] + 1:
+                if n == done[s] + (1 if s == 6 else 1):
+                    flip(s, (S, S) if s == ROUNDS - 1 else (S, S) if s == ROUNDS - 2 else (S, S))
+                    if s % 2 == 1 and s < 7:
+                        recall([s - 1, s])
+            if n == done[ROUNDS - 1] + 1:
+                hold(6)
+            for s in range(ROUNDS):
+                if n == done[s] + (1 if s == 6 else 1):
                     pack(s)
             for s in range(ROUNDS):
-                if n == done[s] + 2:
+                if n == done[s] + (1 if s == 6 else 1) + 1:
                     multiply(s)
                     for bs in parts(s):
                         squash(s, bs)
             for s in range(ROUNDS):
-                if n == whole[s] + 2:
+                if n == whole[s] + 2 and s != 6:
                     hold(s)
             for s in range(ROUNDS):
                 if n == max(done[s] + 2, whole[s] + 2) + 1:
                     for bs in parts(s):
-                        finish(s, bs, ve if s >= 0 else gp)
+                        finish(s, bs, ve)
             for s in range(ROUNDS):
-                if n == done[s] + 2:
+                if n == done[s] + (1 if s == 6 else 1) + 1:
                     for bs in parts(s):
                         lose(s, bs)

@@ -152,31 +152,32 @@ def tile_gcrnncell_pb_kernel(
                 out=ck_plane[32 * quadrant : 32 * quadrant + 4, :].bitcast(F32),
                 in_=c_kernel_scales[0, 4 * quadrant : 4 * quadrant + 4, :].bitcast(F32),
             )
-        G = [[0, 1], [2, 3], [4, 5], [6, 7]]
-        load_support(0, [0])
-        load_support(0, [1])
+        load_support(0, [0, 1])
         load_features([0, 1])
         load_support(1, [0, 1])
         nc.sync.dma_start(
             out=ck_words[:].bitcast(I32),
             in_=c_kernel_words[0].rearrange("p n t -> p (n t)").bitcast(I32),
         )
-        for c in range(1, 4):
-            if c < 3:
-                load_support(0, [2 * c, 2 * c + 1])
-                load_features([2 * c, 2 * c + 1])
-                load_state([2 * c - 2, 2 * c - 1])
-                load_support(1, [2 * c, 2 * c + 1])
-                load_update([2 * c - 2, 2 * c - 1])
-            else:
-                load_support(0, [6, 7])
-                load_features([6, 7])
-                load_state([4, 5])
-                load_support(1, [6])
-                load_update([4, 5])
-                load_support(1, [7])
-                load_state([6, 7])
-                load_update([6, 7])
+        load_support(0, [2, 3])
+        load_features([2, 3])
+        load_state([0, 1])
+        load_support(1, [2, 3])
+        load_update([0, 1])
+        load_support(0, [4, 5])
+        load_features([4, 5])
+        load_state([2, 3])
+        load_support(1, [4, 5])
+        load_update([2, 3])
+        load_support(0, [6, 7])
+        load_features([6, 7])
+        load_state([4, 5])
+        load_update([4, 5])
+        load_support(1, [6])
+        load_support(1, [7])
+        load_state([6, 7])
+        load_update([6, 7])
+
         banks = {"diffused": 2, "flipped": 3, "prev": 1, "product": 2}
 
         r_grouped = keep.tile([P, PASSES, BATCH * UNITS, PACK], BF16, align_bytes=256)
@@ -359,41 +360,55 @@ def tile_gcrnncell_pb_kernel(
         gp, ve = nc.gpsimd, nc.vector
         slots = [(i, s) for group in [[0, 1], [2, 3], [4, 5], [6, 7]] for i in range(SUPPORTS) for s in group]
         done = {s: n for n, (i, s) in enumerate(slots) if i == SUPPORTS - 1}
-        whole = {s: done[group[-1]] for group in [[0, 1], [2, 3], [4, 5], [6, 7]] for s in group}
         def parts(s):
             return single if s >= 6 else [both]
-        for n in range(len(slots) + 5):
+        def flag(s):
+            return done[s] + 1 if s >= 6 else done[s] + 1
+        def mlag(s):
+            return flag(s) + (1 if s >= 6 else (2 if s < 5 else 1))
+        def rlag(s):
+            return flag(s | 1)
+        def hlag(s):
+            return rlag(s) + 0
+        for n in range(len(slots) + 8):
+            if 1 == 0:
+                for s in range(ROUNDS):
+                    if n == mlag(s):
+                        multiply(s)
+                        for bs in parts(s):
+                            squash(s, bs)
             if n < len(slots):
                 diffuse(*slots[n])
                 settle(*slots[n], (S,))
             for s in range(ROUNDS):
-                if n == done[s] - (-1 if s >= 9 else 2):
-                    sort(s, S if s >= 9 and False else V)
-            if n == done[ROUNDS - 1] + 1:
+                if n == max(0, done[s - s % 2] - 2):
+                    sort(s)
+            if n == rlag(7) and 1:
                 recall([6, 7])
             for s in range(ROUNDS):
-                if n == done[s] + (1 if s == 6 else 1):
-                    flip(s, (S, S) if s == ROUNDS - 1 else (S, S) if s == ROUNDS - 2 else (S, S))
-                    if s % 2 == 1 and s < 7:
+                if n == flag(s):
+                    flip(s, (S, S) if s == 7 else (S, V) if s == 6 else (S, S))
+                    if s % 2 == 1 and not (1 and s == 7):
                         recall([s - 1, s])
-            if n == done[ROUNDS - 1] + 1:
+            if n == rlag(7) and 1:
                 hold(6)
             for s in range(ROUNDS):
-                if n == done[s] + (1 if s == 6 else 1):
+                if n == flag(s) + 0:
                     pack(s)
+            if 1 == 1:
+                for s in range(ROUNDS):
+                    if n == mlag(s):
+                        multiply(s)
+                        for bs in parts(s):
+                            squash(s, bs)
             for s in range(ROUNDS):
-                if n == done[s] + (1 if s == 6 else 1) + 1:
-                    multiply(s)
-                    for bs in parts(s):
-                        squash(s, bs)
-            for s in range(ROUNDS):
-                if n == whole[s] + 2 and s != 6:
+                if n == hlag(s) and not (1 and s == 6):
                     hold(s)
             for s in range(ROUNDS):
-                if n == max(done[s] + 2, whole[s] + 2) + 1:
+                if n == max(mlag(s), hlag(s)) + 1:
                     for bs in parts(s):
                         finish(s, bs, ve)
             for s in range(ROUNDS):
-                if n == done[s] + (1 if s == 6 else 1) + 1:
+                if n == mlag(s):
                     for bs in parts(s):
                         lose(s, bs)

from contextlib import ExitStack

import concourse.mybir as mybir
from concourse.masks import make_identity

F32 = mybir.dt.float32
BF16 = mybir.dt.bfloat16
I32 = mybir.dt.int32
U32 = mybir.dt.uint32
U8 = mybir.dt.uint8
FP8X4 = mybir.dt.float8_e4m3fn_x4

P = 128
PACK = 4
K_PASS = P * PACK
BATCH = 2
NODES = 2048
UNITS = 128
SUPPORTS = 2
FEATS = 256
CHANNELS = FEATS + SUPPORTS * UNITS
PASSES = NODES // K_PASS
CHUNK = 512
CHUNKS = NODES // CHUNK
TILES = CHUNK // P
PAIR = 2
PAIRS = TILES // PAIR
ROUND = PAIR * P
ROUNDS = NODES // ROUND

FLOPS = 2 * BATCH * UNITS * NODES * NODES * SUPPORTS + 2 * BATCH * NODES * CHANNELS * UNITS


def tile_gcrnncell_pb_kernel(
    tc,
    r_prev,
    h_diff,
    u,
    state,
    support0_words,
    support0_scales,
    support1_words,
    support1_scales,
    c_kernel_words,
    c_kernel_scales,
    out,
):
    nc = tc.nc
    support_words = (support0_words, support1_words)
    support_scales = (support0_scales, support1_scales)
    tanh = mybir.ActivationFunctionType.Tanh
    alu = mybir.AluOpType

    with ExitStack() as ctx:
        ctx.enter_context(tc.manual_schedule())
        keep = ctx.enter_context(tc.tile_pool(name="keep", bufs=1))
        ring = ctx.enter_context(tc.tile_pool(name="ring", bufs=2))
        psum = ctx.enter_context(tc.psum_pool(name="psum", bufs=1))

        w_plane = [
            keep.tile([P, NODES], U8, name="w_plane%d" % i, align_bytes=256) for i in range(SUPPORTS)
        ]
        for i in range(SUPPORTS):
            nc.vector.memset(w_plane[i][:].bitcast(I32), 0)
        ck_words = keep.tile([P, UNITS], U32, align_bytes=256)
        ck_plane = keep.tile([P, UNITS], U8, align_bytes=256)
        nc.vector.memset(ck_plane[:].bitcast(I32), 0)
        warm = keep.tile([P, 1], F32, align_bytes=256)
        nc.vector.memset(warm[:], 0.0)
        nc.scalar.activation(out=warm[:], in_=warm[:], func=tanh)
        identity = keep.tile([P, P], F32, align_bytes=256)
        make_identity(nc, identity[:])
        sorter = keep.tile([P, P], F32, align_bytes=256)
        nc.vector.tensor_copy(
            out=sorter[:].rearrange("p (v x e) -> p v x e", v=2, e=2),
            in_=identity[:].rearrange("p (x v e) -> p v x e", v=2, e=2),
        )

        w_words = {}
        hc = {}
        h_raw = {}
        state_sb = {}
        u_sb = {}

        def load_support(i, rounds):
            words = keep.tile(
                [P, PASSES, len(rounds) * ROUND],
                U32,
                name="w_words%d_%d" % (i, rounds[0]),
                align_bytes=256,
            )
            nc.sync.dma_start(
                out=words[:].bitcast(I32),
                in_=support_words[i]
                .rearrange("g p n t -> p g (n t)")
                .bitcast(I32)[:, :, rounds[0] * ROUND : (rounds[-1] + 1) * ROUND],
            )
            for n, s in enumerate(rounds):
                w_words[i, s] = words[:, :, n * ROUND : (n + 1) * ROUND]

        def load_features(rounds):
            for s in rounds:
                hc[s] = keep.tile([P, PAIR, BATCH, 2, CHANNELS // 2], BF16, name="hc%d" % s, align_bytes=256)
            raw = keep.tile(
                [P, PAIR * len(rounds), BATCH, FEATS], BF16, name="h_raw%d" % rounds[0], align_bytes=256)
            for b in range(BATCH):
                nc.sync.dma_start(
                    out=raw[:, :, b, :],
                    in_=h_diff[b, rounds[0] * ROUND : (rounds[-1] + 1) * ROUND, :].rearrange(
                        "(t x) f -> x t f", x=P
                    ),
                )
            for n, s in enumerate(rounds):
                h_raw[s] = raw[:, PAIR * n : PAIR * (n + 1)]

        def load_state(rounds):
            tile = keep.tile([P, BATCH, len(rounds) * ROUND], BF16, name="state%d" % rounds[0], align_bytes=256)
            nc.sync.dma_start(
                out=tile[:],
                in_=state.rearrange("b (k n) -> k b n", n=NODES)[
                    :, :, rounds[0] * ROUND : (rounds[-1] + 1) * ROUND
                ],
            )
            for n, s in enumerate(rounds):
                state_sb[s] = tile[:, :, n * ROUND : (n + 1) * ROUND]

        def load_update(rounds):
            tile = keep.tile(
                [P, len(rounds), BATCH, PAIR * UNITS], BF16, name="u%d" % rounds[0], align_bytes=256)
            for b in range(BATCH):
                nc.sync.dma_start(
                    out=tile[:, :, b, :],
                    in_=u[b, rounds[0] * ROUND : (rounds[-1] + 1) * ROUND, :].rearrange(
                        "(r x j) k -> x r (j k)", x=P, j=PAIR
                    ),
                )
            for n, s in enumerate(rounds):
                u_sb[s] = tile[:, n]

        r_sb = keep.tile([P, BATCH, NODES], BF16, align_bytes=256)
        for part in range(2):
            cols = slice(part * NODES // 2, (part + 1) * NODES // 2)
            nc.sync.dma_start(out=r_sb[:, :, cols], in_=r_prev.rearrange("b k n -> k b n")[:, :, cols])
        for i in range(SUPPORTS):
            for quadrant in range(4):
                nc.gpsimd.dma_start(
                    out=w_plane[i][32 * quadrant : 32 * quadrant + 16, :].bitcast(F32),
                    in_=support_scales[i][:, 4 * quadrant : 4 * quadrant + 4, :].bitcast(F32),
                )
        for quadrant in range(4):
            nc.gpsimd.dma_start(
                out=ck_plane[32 * quadrant : 32 * quadrant + 4, :].bitcast(F32),
                in_=c_kernel_scales[0, 4 * quadrant : 4 * quadrant + 4, :].bitcast(F32),
            )
        load_support(0, [0, 1])
        load_features([0, 1])
        load_support(1, [0, 1])
        nc.sync.dma_start(
            out=ck_words[:].bitcast(I32),
            in_=c_kernel_words[0].rearrange("p n t -> p (n t)").bitcast(I32),
        )
        load_support(0, [2, 3])
        load_features([2, 3])
        load_state([0, 1])
        load_support(1, [2, 3])
        load_update([0, 1])
        load_support(0, [4, 5])
        load_features([4, 5])
        load_state([2, 3])
        load_support(1, [4, 5])
        load_update([2, 3])
        load_support(0, [6, 7])
        load_features([6, 7])
        load_state([4, 5])
        load_update([4, 5])
        load_support(1, [6])
        load_support(1, [7])
        load_state([6, 7])
        load_update([6, 7])

        banks = {"diffused": 2, "flipped": 3, "prev": 1, "product": 2}

        r_grouped = keep.tile([P, PASSES, BATCH * UNITS, PACK], BF16, align_bytes=256)
        r_words = keep.tile([P, PASSES, BATCH * UNITS], U32, align_bytes=256)
        r_plane = keep.tile([P, PASSES, BATCH * UNITS], U8, align_bytes=256)

        def r_flip(g):
            r_flipped = psum.tile(
                [P, 2, BATCH, UNITS], F32, tag="flipped", bufs=banks["flipped"], name="r_flipped"
            )
            for b in range(BATCH):
                for half in range(2):
                    nc.tensor.transpose(
                        r_flipped[:, half, b, :],
                        r_sb[:, b, :].bitcast(F32)[:, 256 * g + half : 256 * (g + 1) : 2],
                        sorter[:],
                    )
            copy = nc.vector.tensor_copy if g % 2 == 0 else nc.scalar.copy
            copy(out=r_grouped[:, g].bitcast(F32), in_=r_flipped[:].rearrange("p h b k -> p (b k) h"))

        def r_pack(g):
            nc.vector.quantize_mx(
                out=r_words[:, g, :].bitcast(FP8X4),
                scales=r_plane[:, g, :],
                in_=r_grouped[:, g].rearrange("p c t -> p (c t)"),
            )

        hc_grouped = {}
        hc_packed = {}
        diffused = {}
        prev = {}
        kept = {}
        product = {}
        fresh = {}
        lost = {}
        z = {}

        def sort(s, engine=nc.vector.tensor_copy):
            engine(
                out=hc[s][:, :, :, :, 0 : FEATS // 2].bitcast(F32).rearrange("p t b v w -> p (t b) v w"),
                in_=h_raw[s]
                .rearrange("p t b f -> p (t b f)")
                .bitcast(F32)
                .rearrange("p (c w v) -> p c v w", v=2, w=FEATS // 4),
            )

        def diffuse(i, s):
            diffused[i, s] = psum.tile(
                [P, PAIR, BATCH * UNITS], F32, tag="diffused", bufs=banks["diffused"], name="diffused"
            )
            for t in range(PAIR):
                first = t * P
                for g in range(PASSES):
                    nc.tensor.matmul_mx(
                        out=diffused[i, s][:, t, :],
                        lhsT=w_words[i, s][:, g, first : first + P].bitcast(FP8X4),
                        lhsT_scale=w_plane[i][4 * g : P, s * ROUND + first : s * ROUND + first + P],
                        rhs=r_words[:, g, :].bitcast(FP8X4),
                        rhs_scale=r_plane[:, g, :],
                        start=(g == 0),
                        stop=(g == PASSES - 1),
                    )

        def settle(i, s, engines):
            first = FEATS // 2 + i * UNITS // 2
            for n, engine in enumerate(engines):
                ts = slice(n * PAIR // len(engines), (n + 1) * PAIR // len(engines))
                engine(
                    out=hc[s][:, ts, :, :, first : first + UNITS // 2].rearrange(
                        "p t b v k -> p (t b v) k"
                    ),
                    in_=diffused[i, s][:, ts].rearrange("p t (c k) -> p (t c) k", k=UNITS // 2),
                )

        def flip(s, engines):
            grouped = ring.tile([P, BATCH, PAIR, P, PACK], BF16, align_bytes=256, name="hc_grouped")
            for b in range(BATCH):
                flipped = psum.tile([P, 2, ROUND], F32, tag="flipped", bufs=banks["flipped"], name="flipped")
                for t in range(PAIR):
                    for half in range(2):
                        nc.tensor.transpose(
                            flipped[:, half, t * P : (t + 1) * P],
                            hc[s][:, t, b, half, :].bitcast(F32),
                            identity[:],
                        )
                engines[b](
                    out=grouped[:, b].bitcast(F32),
                    in_=flipped[:].rearrange("p h (x j) -> p j x h", j=PAIR),
                )
            hc_grouped[s] = grouped
            hc_packed[s] = (
                ring.tile([P, BATCH, PAIR, P], U32, align_bytes=256, name="hc_words"),
                ring.tile([P, BATCH, PAIR, P], U8, align_bytes=256, name="hc_plane"),
            )

        def pack(s):
            words, plane = hc_packed[s]
            for b in range(BATCH):
                nc.vector.quantize_mx(
                    out=words[:, b].rearrange("p j x -> p (j x)").bitcast(FP8X4),
                    scales=plane[:, b].rearrange("p j x -> p (j x)"),
                    in_=hc_grouped[s][:, b].rearrange("p j x t -> p (j x t)"),
                )

        def recall(rounds):
            tile = psum.tile([P, 2, BATCH, UNITS], F32, tag="prev", bufs=banks["prev"], name="prev")
            for n, s in enumerate(rounds):
                prev[s] = tile[:, n]
                for b in range(BATCH):
                    nc.tensor.transpose(
                        tile[:, n, b, :],
                        state_sb[s][:, b, :].bitcast(F32),
                        identity[:],
                    )

        def hold(s):
            kept[s] = ring.tile([P, BATCH, PAIR, UNITS], F32, name="kept", bufs=3, align_bytes=256)
            nc.vector.tensor_tensor(
                out=kept[s][:],
                in0=prev[s]
                .rearrange("p b k -> p (b k)")
                .bitcast(BF16)
                .rearrange("p (b k j) -> p b j k", b=BATCH, j=PAIR),
                in1=u_sb[s].rearrange("p b (j k) -> p b j k", j=PAIR),
                op=alu.mult,
            )

        def multiply(s):
            product[s] = psum.tile([P, BATCH, PAIR, UNITS], F32, tag="product", bufs=banks["product"], name="product")
            words, plane = hc_packed[s]
            fresh[s] = ring.tile([P, BATCH, PAIR * UNITS], F32, name="fresh", align_bytes=256)
            lost[s] = ring.tile([P, BATCH, PAIR * UNITS], F32, name="lost", align_bytes=256)
            z[s] = keep.tile([P, BATCH, PAIR * UNITS], F32, name="z%d" % s, align_bytes=256)
            for b in range(BATCH):
                for j in range(PAIR):
                    nc.tensor.matmul_mx(
                        out=product[s][:, b, j, :],
                        lhsT=words[:, b, j, :].bitcast(FP8X4),
                        lhsT_scale=plane[:, b, j, :],
                        rhs=ck_words[:].bitcast(FP8X4),
                        rhs_scale=ck_plane[:],
                        start=True,
                        stop=True,
                    )

        def squash(s, bs):
            nc.scalar.activation(
                out=fresh[s][:, bs], in_=product[s][:, bs].rearrange("p b j k -> p b (j k)"), func=tanh
            )

        def lose(s, bs):
            nc.vector.scalar_tensor_tensor(
                out=lost[s][:, bs],
                in0=u_sb[s][:, bs],
                scalar=1.0,
                in1=fresh[s][:, bs],
                op0=alu.subtract,
                op1=alu.mult,
            )

        out_view = out.rearrange("b (s x f) -> s x b f", s=ROUNDS, x=P)

        def finish(s, bs, engine):
            engine.tensor_tensor(
                out=z[s][:, bs],
                in0=kept[s][:, bs].rearrange("p b j k -> p b (j k)"),
                in1=lost[s][:, bs],
                op=alu.subtract,
            )
            nc.sync.dma_start(out=out_view[s][:, bs], in_=z[s][:, bs])

        for g in range(PASSES):
            r_flip(g)
            if g % 2 == 1:
                r_pack(g - 1)
                r_pack(g)
        V, S = nc.vector.tensor_copy, nc.scalar.copy
        both = slice(0, BATCH)
        single = [slice(b, b + 1) for b in range(BATCH)]
        gp, ve = nc.gpsimd, nc.vector
        slots = [(i, s) for group in [[0, 1], [2, 3], [4, 5], [6, 7]] for i in range(SUPPORTS) for s in group]
        done = {s: n for n, (i, s) in enumerate(slots) if i == SUPPORTS - 1}
        def parts(s):
            return single if s >= 6 else [both]
        def flag(s):
            return done[s] + 1 if s >= 6 else done[s] + 1
        def mlag(s):
            return flag(s) + (1 if s >= 6 else (2 if s < 5 else 1))
        def rlag(s):
            return flag(s | 1)
        def hlag(s):
            return rlag(s) + 0
        for n in range(len(slots) + 8):
            if 1 == 0:
                for s in range(ROUNDS):
                    if n == mlag(s):
                        multiply(s)
                        for bs in parts(s):
                            squash(s, bs)
            if n < len(slots):
                diffuse(*slots[n])
                settle(*slots[n], (S,))
            for s in range(ROUNDS):
                if n == max(0, done[s - s % 2] - 2):
                    sort(s)
            if n == rlag(7) and 1:
                recall([6, 7])
            for s in range(ROUNDS):
                if n == flag(s):
                    flip(s, (S, S) if s == 7 else (S, V) if s == 6 else (S, S))
                    if s % 2 == 1 and not (1 and s == 7):
                        recall([s - 1, s])
            if n == rlag(7) and 1:
                hold(6)
            for s in range(ROUNDS):
                if n == flag(s) + 0:
                    pack(s)
            if 1 == 1:
                for s in range(ROUNDS):
                    if n == mlag(s):
                        multiply(s)
                        for bs in parts(s):
                            squash(s, bs)
            for s in range(ROUNDS):
                if n == hlag(s) and not (1 and s == 6):
                    hold(s)
            for s in range(ROUNDS):
                if n == max(mlag(s), hlag(s)) + 1:
                    for bs in parts(s):
                        finish(s, bs, ve)
            for s in range(ROUNDS):
                if n == mlag(s):
                    for bs in parts(s):
                        lose(s, bs)
